import numpy as np
import ml_dtypes


def mxq(x, axis, fmt="e4m3"):
    dtype, down = {"e4m3": (ml_dtypes.float8_e4m3fn, 7), "e5m2": (ml_dtypes.float8_e5m2, 14)}[fmt]
    v = np.moveaxis(np.asarray(x, np.float32).astype(ml_dtypes.bfloat16).astype(np.float64), axis, -1)
    blocks = v.reshape(v.shape[:-1] + (-1, 32))
    amax = np.abs(blocks).max(-1, keepdims=True)
    byte = np.maximum(np.where(amax > 0, np.frexp(amax)[1] - 1 + 127, 0) - down, 1)
    scale = np.exp2(byte - 127.0)
    codes = (blocks / scale).astype(np.float32).astype(dtype).astype(np.float64)
    return np.moveaxis((codes * scale).reshape(v.shape), -1, axis)


WIDE = False


def mx_kscale(k):
    if not WIDE:
        return np.ones(k)
    levels = np.array([10, -10, 5, -5, 0])
    if k % 512:
        return np.exp2(np.random.permutation(np.resize(levels, k // 32))).repeat(32)
    a = np.empty((k // 512, 16))
    for p in range(k // 512):
        a[p, :8] = np.random.permutation(np.resize(levels, 8))
        for g in range(8):
            far = levels[np.abs(levels - a[p, g]) >= 10]
            a[p, g + 8] = far[np.random.randint(len(far))]
    return np.exp2(a.ravel()).repeat(32)


BF16 = ml_dtypes.bfloat16


def bf(x):
    return np.asarray(x, np.float32).astype(BF16)


def f64(x):
    return np.asarray(x).astype(np.float64)


B, S, DIM, H, NOPE, ROPE_D, VD = 2, 128, 2048, 16, 128, 64, 128
QKD = NOPE + ROPE_D
BASE = 10000.0


def rope_cos_sin(seq_len):
    theta = 1.0 / BASE ** (f64(np.arange(0, ROPE_D, 2)) / ROPE_D)
    pos = f64(np.arange(seq_len))
    ang = pos[:, None] * theta[None, :]
    return np.cos(ang), np.sin(ang)


def apply_rope(v, cos, sin):
    b, s, h, d = v.shape
    vs = v.reshape(b, s, h, d // 2, 2)
    c = cos[None, :, None, :]
    sn = sin[None, :, None, :]
    out = np.stack([vs[..., 0] * c - vs[..., 1] * sn, vs[..., 1] * c + vs[..., 0] * sn], axis=-1)
    return out.reshape(b, s, h, d)


def draw0():
    s = mx_kscale(DIM)
    return {'x': bf(np.random.standard_normal((B, S, DIM)) * s),
            'Wq': bf(np.random.standard_normal((DIM, H * QKD)) / np.sqrt(DIM) / s[:, None]),
            'Wk': bf(np.random.standard_normal((DIM, H * QKD)) / np.sqrt(DIM) / s[:, None])}


def core(x, Wq, Wk):
    xq = mxq(f64(x), 2, 'e4m3')
    q = (xq @ mxq(f64(Wq), 0, 'e4m3')).reshape(B, S, H, QKD)
    k = (xq @ mxq(f64(Wk), 0, 'e4m3')).reshape(B, S, H, QKD)
    cos, sin = rope_cos_sin(S)
    q = np.concatenate([q[..., :NOPE], apply_rope(q[..., NOPE:], cos, sin)], axis=-1)
    k = np.concatenate([k[..., :NOPE], apply_rope(k[..., NOPE:], cos, sin)], axis=-1)
    return q, k


def e4m3fn_bytes(y):
    return np.clip(np.asarray(y, np.float64), -448.0, 448.0).astype(np.float32).astype(ml_dtypes.float8_e4m3fn).view(np.uint8)


def e4m3fn_values(b):
    return np.asarray(b, np.uint8).view(ml_dtypes.float8_e4m3fn).astype(np.float64)


def setup_inputs():
    d = draw0()
    x0 = np.asarray(d['Wq']).astype(np.float64)
    s = (np.max(np.abs(x0), axis=(1,), keepdims=True) / 448.0).astype(np.float32)
    out = {}
    for k, v in d.items():
        if k == 'Wq':
            out['Wq_bytes'] = e4m3fn_bytes(x0 / s.astype(np.float64))
            out['Wq_scale'] = s
        else:
            out[k] = v
    return out


def reference(x, Wq_bytes, Wq_scale, Wk):
    return core(x, e4m3fn_values(Wq_bytes) * Wq_scale.astype(np.float64), Wk)

@@ -1,0 +1,302 @@
+from contextlib import ExitStack
+import math
+
+import concourse.mybir as mybir
+from concourse.masks import make_identity
+
+FLOPS = 2 * 256 * 2048 * 6144
+
+F32 = mybir.dt.float32
+BF16 = mybir.dt.bfloat16
+I32 = mybir.dt.int32
+U32 = mybir.dt.uint32
+U8 = mybir.dt.uint8
+FP8 = mybir.dt.float8_e4m3fn
+FP8X4 = mybir.dt.float8_e4m3fn_x4
+ALU = mybir.AluOpType
+ACT = mybir.ActivationFunctionType
+
+P = 128
+PACK = 4
+PASSES = 4
+SEQS = 2
+NOPE = 128
+ROPE = 64
+HEAD = NOPE + ROPE
+PAIRS = ROPE // 2
+CH_HEADS = 4
+CHUNK = CH_HEADS * HEAD
+CHUNKS = 4
+ROUNDS = CHUNKS * PASSES
+UNIT = 512
+HALF = UNIT // 2
+AHEAD = 4
+X_ROUND = 2
+CODE_BUFS = 10
+RATIO = 10000.0 ** (-2.0 / ROPE)
+S_NOPE = (("q", 4), ("q", 8), ("q", 12), ("q", 15), ("k", 15))
+
+
+def tile_mla_pa_kernel(tc, x, Wq_bytes, Wq_scale, Wk, out_0, out_1):
+    nc = tc.nc
+    wk_rows = Wk.rearrange("(g p t) n -> g p t n", p=P, t=PACK)
+    wq_rows = Wq_bytes.rearrange("(g p t) n -> g p t n", p=P, t=PACK)
+    outs = (
+        out_0.rearrange("b s h f -> b s (h f)"),
+        out_1.rearrange("b s h f -> b s (h f)"),
+    )
+
+    with ExitStack() as ctx:
+        sb = ctx.enter_context(tc.tile_pool(name="sb", bufs=1))
+        ps = ctx.enter_context(tc.psum_pool(name="ps", bufs=1))
+        ctx.enter_context(tc.manual_schedule())
+
+        q_bytes = {}
+        k_raw = {}
+        q_wide = {}
+        grouped = {}
+        codes = {}
+        acc = {}
+        res = {}
+        products = []
+
+        def load(r):
+            c, g = divmod(r, PASSES)
+            cols = slice(c * CHUNK, (c + 1) * CHUNK)
+            q_bytes[r] = sb.tile([P, PACK, CHUNK], U8, name="q_bytes", tag="q_bytes", bufs=AHEAD + 1)
+            nc.sync.dma_start(out=q_bytes[r][:], in_=wq_rows[g][:, :, cols])
+            k_raw[r] = sb.tile([P, PACK, CHUNK], BF16, name="k_raw", tag="k_raw", bufs=AHEAD + 1)
+            nc.sync.dma_start(out=k_raw[r][:], in_=wk_rows[g][:, :, cols])
+
+        q_scale = sb.tile([P, PASSES, PACK], F32, name="q_scale", tag="q_scale")
+        nc.sync.dma_start(out=q_scale[:], in_=Wq_scale.rearrange("(g p t) o -> p g (t o)", p=P, t=PACK))
+        load(0)
+        load(1)
+        x_raw = sb.tile([P, SEQS, PASSES * P * PACK], BF16, name="x_raw", tag="x_raw")
+        for m in range(SEQS):
+            nc.sync.dma_start(out=x_raw[:, m, :], in_=x[m])
+        load(2)
+        load(3)
+
+        pos = sb.tile([P, 1], F32, name="pos", tag="pos")
+        nc.gpsimd.iota(pos[:], pattern=[[0, 1]], base=0, channel_multiplier=1, allow_small_or_imprecise_dtypes=True)
+        ident = sb.tile([P, P], F32, name="ident", tag="ident")
+        make_identity(nc, ident[:])
+
+        zero = sb.tile([P, 1], F32, name="zero", tag="zero")
+        warm = sb.tile([P, 1], F32, name="warm", tag="warm")
+        nc.vector.memset(zero[:], 0.0)
+        nc.scalar.activation(out=warm[:], in_=zero[:], func=ACT.Sin)
+
+        turns = sb.tile([P, 2, PAIRS], F32, name="turns", tag="turns")
+        nc.vector.tensor_scalar(out=turns[:, 1, 0:1], in0=pos[:], scalar1=1.0 / (2.0 * math.pi), scalar2=None, op0=ALU.mult)
+        w = 1
+        while w < PAIRS:
+            nc.vector.tensor_scalar(out=turns[:, 1, w:2 * w], in0=turns[:, 1, 0:w], scalar1=RATIO ** w, scalar2=None, op0=ALU.mult)
+            w *= 2
+        nc.vector.tensor_scalar(out=turns[:, 0, :], in0=turns[:, 1, :], scalar1=0.25, scalar2=None, op0=ALU.add)
+        turns_flat = turns[:].rearrange("p a i -> p (a i)")
+        whole_i = sb.tile([P, 2 * PAIRS], I32, name="whole_i", tag="whole_i")
+        whole_f = sb.tile([P, 2 * PAIRS], F32, name="whole_f", tag="whole_f")
+        frac = sb.tile([P, 2 * PAIRS], F32, name="frac", tag="frac")
+        minus = sb.tile([P, 2 * PAIRS], F32, name="minus", tag="minus")
+        nc.vector.tensor_copy(out=whole_i[:], in_=turns_flat)
+        nc.vector.tensor_copy(out=whole_f[:], in_=whole_i[:])
+        nc.vector.tensor_tensor(out=frac[:], in0=turns_flat, in1=whole_f[:], op=ALU.subtract)
+        nc.vector.scalar_tensor_tensor(out=minus[:], in0=frac[:], scalar=0.5, in1=frac[:], op0=ALU.is_gt, op1=ALU.subtract)
+        cos_sin = sb.tile([P, 2, PAIRS], F32, name="cos_sin", tag="cos_sin")
+        nc.scalar.activation(out=cos_sin[:].rearrange("p a i -> p (a i)"), in_=minus[:], func=ACT.Sin, scale=-2.0 * math.pi)
+        table = sb.tile([P, 2, UNIT], F32, name="table", tag="table")
+
+        def finish_tables():
+            first = table[:, :, 0:ROPE].rearrange("p a (i two) -> p a i two", two=2)
+            nc.vector.tensor_copy(out=first[:, :, :, 0], in_=cos_sin[:])
+            nc.vector.tensor_copy(out=first[:, 0, :, 1], in_=cos_sin[:, 0, :])
+            nc.vector.tensor_scalar(out=first[:, 1, :, 1], in0=cos_sin[:, 1, :], scalar1=-1.0, scalar2=None, op0=ALU.mult)
+            n = ROPE
+            while n < UNIT:
+                nc.vector.tensor_copy(out=table[:, :, n:2 * n], in_=table[:, :, 0:n])
+                n *= 2
+
+        x_words = sb.tile([P, SEQS, PASSES, P, 2], F32, name="x_words", tag="x_words", align_bytes=64)
+        x_codes = sb.tile([P, SEQS * PASSES * P], U32, name="x_codes", tag="x_codes", align_bytes=64)
+        x_scales = sb.tile([P, SEQS * PASSES * P], U8, name="x_scales", tag="x_scales", align_bytes=64)
+        x_turned = {}
+        for m in range(SEQS):
+            words = x_raw[:, m, :].bitcast(F32)
+            for gp in range(PASSES // 2):
+                x_turned[(m, gp)] = ps.tile([P, 4, P], F32, name="x_turned", tag="bank", bufs=8)
+                for gl in range(2):
+                    g = 2 * gp + gl
+                    for u in range(2):
+                        nc.tensor.transpose(
+                            x_turned[(m, gp)][:, 2 * gl + u, :],
+                            words[:, 2 * P * g + u:2 * P * (g + 1):2],
+                            ident[:],
+                        )
+
+        def copy_x():
+            for m in range(SEQS):
+                for gp in range(PASSES // 2):
+                    nc.scalar.copy(
+                        out=x_words[:, m, 2 * gp:2 * gp + 2, :, :],
+                        in_=x_turned[(m, gp)][:].rearrange("p (g u) r -> p g r u", u=2),
+                    )
+
+        def quantize_x():
+            nc.vector.quantize_mx(
+                out=x_codes[:].bitcast(FP8X4),
+                scales=x_scales[:],
+                in_=x_words[:].rearrange("p m g r u -> p (m g r u)").bitcast(BF16),
+            )
+
+        def by_head(tile_ap, lo, hi):
+            return tile_ap.rearrange("p t (h f) -> p h f t", f=HEAD)[:, :, lo:hi, :]
+
+        def open_round(r):
+            q_wide[r] = sb.tile([P, PACK, CHUNK], BF16, name="q_wide", tag="q_wide", bufs=3)
+            grouped[("r", r)] = sb.tile([P, UNIT, PACK], BF16, name="grp_r", tag="grp_r", bufs=3, align_bytes=64)
+
+        def widen(r, t, on_vector):
+            g = r % PASSES
+            src = q_bytes[r][:, t, :].bitcast(FP8)
+            if on_vector:
+                nc.vector.tensor_scalar(out=q_wide[r][:, t, :], in0=src, scalar1=q_scale[:, g, t:t + 1], scalar2=None, op0=ALU.mult)
+            else:
+                nc.scalar.activation(out=q_wide[r][:, t, :], in_=src, func=ACT.Copy, scale=q_scale[:, g, t:t + 1])
+
+        def rope_dst(r, first):
+            return grouped[("r", r)][:, first:first + HALF, :].rearrange("p (h f) t -> p h f t", f=ROPE)
+
+        def widen_round(r):
+            open_round(r)
+            for t in range(PACK):
+                widen(r, t, False)
+            nc.scalar.copy(out=rope_dst(r, 0), in_=by_head(q_wide[r][:], NOPE, HEAD))
+            for kind in ("k", "q"):
+                if (kind, r) in S_NOPE:
+                    interleave_nope(kind, r, nc.scalar.copy)
+
+        def interleave_nope(kind, r, copy):
+            src = k_raw[r] if kind == "k" else q_wide[r]
+            grouped[(kind, r)] = sb.tile([P, UNIT, PACK], BF16, name="grp_" + kind, tag="grp_" + kind, bufs=3, align_bytes=64)
+            copy(
+                out=grouped[(kind, r)][:].rearrange("p (h f) t -> p h f t", f=NOPE),
+                in_=by_head(src[:], 0, NOPE),
+            )
+
+        def quantize(kind, r):
+            cd = sb.tile([P, UNIT], U32, name="codes", tag="codes", bufs=CODE_BUFS, align_bytes=64)
+            sl = sb.tile([P, UNIT], U8, name="scales", tag="scales", bufs=CODE_BUFS, align_bytes=64)
+            nc.vector.quantize_mx(
+                out=cd[:].bitcast(FP8X4),
+                scales=sl[:],
+                in_=grouped[(kind, r)][:].rearrange("p c t -> p (c t)"),
+            )
+            codes[(kind, r)] = (cd, sl)
+            products.append((kind, r))
+
+        def multiply(kind, r):
+            g = r % PASSES
+            cd, sl = codes[(kind, r)]
+            for m in range(SEQS):
+                if g == 0:
+                    acc[(kind, m)] = ps.tile([P, UNIT], F32, name="acc", tag="bank", bufs=8)
+                xcols = slice((m * PASSES + g) * P, (m * PASSES + g + 1) * P)
+                nc.tensor.matmul_mx(
+                    out=acc[(kind, m)][:],
+                    lhsT=x_codes[:, xcols].bitcast(FP8X4),
+                    lhsT_scale=x_scales[:, xcols],
+                    rhs=cd[:].bitcast(FP8X4),
+                    rhs_scale=sl[:],
+                    start=(g == 0),
+                    stop=(g == PASSES - 1),
+                )
+
+        def flush_products():
+            for kind, r in products:
+                multiply(kind, r)
+            products.clear()
+
+        def copy_nope(kind, m):
+            first = 0 if kind == "q" else CH_HEADS
+            nc.scalar.copy(
+                out=res[m][:, first:first + CH_HEADS, 0:NOPE],
+                in_=acc[(kind, m)][:].rearrange("p (h f) -> p h f", f=NOPE),
+            )
+
+        def rotate(m):
+            bank = acc[("r", m)]
+            crossed = sb.tile([P, UNIT], F32, name="crossed", tag="crossed", bufs=2)
+            nc.vector.tensor_tensor(out=crossed[:], in0=bank[:], in1=table[:, 1, :], op=ALU.mult)
+            nc.vector.tensor_tensor(
+                out=res[m][:, :, NOPE:HEAD],
+                in0=bank[:].rearrange("p (h f) -> p h f", f=ROPE),
+                in1=table[:, 0, :].rearrange("p (h f) -> p h f", f=ROPE),
+                op=ALU.mult,
+            )
+            pairs = res[m][:, :, NOPE:HEAD].rearrange("p h (i two) -> p h i two", two=2)
+            nc.vector.tensor_tensor(
+                out=pairs,
+                in0=pairs,
+                in1=crossed[:].rearrange("p (h i two) -> p h i two", i=PAIRS, two=2)[:, :, :, ::-1],
+                op=ALU.add,
+            )
+
+        def store(c, m):
+            cols = slice(c * CHUNK, (c + 1) * CHUNK)
+            for wi in (1, 0):
+                nc.sync.dma_start(
+                    out=outs[wi][m, :, cols],
+                    in_=res[m][:, wi * CH_HEADS:(wi + 1) * CH_HEADS, :].rearrange("p h f -> p (h f)"),
+                )
+
+        open_round(0)
+        widen(0, 0, False)
+        widen(0, 1, False)
+        widen(0, 2, True)
+        widen(0, 3, True)
+
+        for r in range(ROUNDS + 1):
+            closed = r > 0 and r % PASSES == 0
+            if closed:
+                for m in range(SEQS):
+                    res[m] = sb.tile([P, 2 * CH_HEADS, HEAD], F32, name="res", tag="res", bufs=4)
+            if r + AHEAD < ROUNDS:
+                load(r + AHEAD)
+            if closed:
+                for m in range(SEQS):
+                    copy_nope("k", m)
+            if r + 1 < ROUNDS:
+                widen_round(r + 1)
+            if r == X_ROUND - 1:
+                copy_x()
+            if r < ROUNDS:
+                nc.vector.tensor_copy(out=rope_dst(r, HALF), in_=by_head(k_raw[r][:], NOPE, HEAD))
+            if r > 0:
+                quantize("q", r - 1)
+            if r == X_ROUND:
+                quantize_x()
+            if r >= X_ROUND:
+                flush_products()
+            if closed:
+                for m in range(SEQS):
+                    rotate(m)
+                for m in range(SEQS):
+                    copy_nope("q", m)
+                for m in range(SEQS):
+                    store(r // PASSES - 1, m)
+            if r < ROUNDS:
+                if ("k", r) not in S_NOPE:
+                    interleave_nope("k", r, nc.vector.tensor_copy)
+                if r == 0:
+                    finish_tables()
+                    nc.vector.tensor_copy(out=rope_dst(0, 0), in_=by_head(q_wide[0][:], NOPE, HEAD))
+                quantize("r", r)
+                if r >= X_ROUND:
+                    flush_products()
+                if ("q", r) not in S_NOPE:
+                    interleave_nope("q", r, nc.vector.tensor_copy)
+                quantize("k", r)
+                if r >= X_ROUND:
+                    flush_products()

@@ -31,6 +31,7 @@ ROUNDS = CHUNKS * PASSES
 UNIT = 512
 HALF = UNIT // 2
 AHEAD = 4
+RUN = 4
 X_ROUND = 2
 CODE_BUFS = 10
 RATIO = 10000.0 ** (-2.0 / ROPE)
@@ -151,7 +152,8 @@ def tile_mla_pa_kernel(tc, x, Wq_bytes, Wq_scale, Wk, out_0, out_1):
             )
 
         def by_head(tile_ap, lo, hi):
-            return tile_ap.rearrange("p t (h f) -> p h f t", f=HEAD)[:, :, lo:hi, :]
+            picked = tile_ap.rearrange("p t (h f) -> p h f t", f=HEAD)[:, :, lo:hi, :]
+            return picked.rearrange("p h (c i) t -> p h c t i", i=RUN)
 
         def open_round(r):
             q_wide[r] = sb.tile([P, PACK, CHUNK], BF16, name="q_wide", tag="q_wide", bufs=3)
@@ -166,7 +168,7 @@ def tile_mla_pa_kernel(tc, x, Wq_bytes, Wq_scale, Wk, out_0, out_1):
                 nc.scalar.activation(out=q_wide[r][:, t, :], in_=src, func=ACT.Copy, scale=q_scale[:, g, t:t + 1])
 
         def rope_dst(r, first):
-            return grouped[("r", r)][:, first:first + HALF, :].rearrange("p (h f) t -> p h f t", f=ROPE)
+            return grouped[("r", r)][:, first:first + HALF, :].rearrange("p (h c i) t -> p h c t i", h=CH_HEADS, i=RUN)
 
         def widen_round(r):
             open_round(r)
@@ -181,7 +183,7 @@ def tile_mla_pa_kernel(tc, x, Wq_bytes, Wq_scale, Wk, out_0, out_1):
             src = k_raw[r] if kind == "k" else q_wide[r]
             grouped[(kind, r)] = sb.tile([P, UNIT, PACK], BF16, name="grp_" + kind, tag="grp_" + kind, bufs=3, align_bytes=64)
             copy(
-                out=grouped[(kind, r)][:].rearrange("p (h f) t -> p h f t", f=NOPE),
+                out=grouped[(kind, r)][:].rearrange("p (h c i) t -> p h c t i", h=CH_HEADS, i=RUN),
                 in_=by_head(src[:], 0, NOPE),
             )
 

@@ -35,7 +35,7 @@ RUN = 4
 X_ROUND = 2
 CODE_BUFS = 10
 RATIO = 10000.0 ** (-2.0 / ROPE)
-S_NOPE = (("q", 4), ("q", 8), ("q", 12), ("q", 15), ("k", 15))
+S_NOPE = (("q", 4), ("q", 8), ("q", 10), ("q", 12), ("q", 14), ("q", 15), ("k", 15))
 
 
 def tile_mla_pa_kernel(tc, x, Wq_bytes, Wq_scale, Wk, out_0, out_1):
@@ -60,6 +60,7 @@ def tile_mla_pa_kernel(tc, x, Wq_bytes, Wq_scale, Wk, out_0, out_1):
         acc = {}
         res = {}
         products = []
+        passed = {}
 
         def load(r):
             c, g = divmod(r, PASSES)
@@ -83,6 +84,8 @@ def tile_mla_pa_kernel(tc, x, Wq_bytes, Wq_scale, Wk, out_0, out_1):
         nc.gpsimd.iota(pos[:], pattern=[[0, 1]], base=0, channel_multiplier=1, allow_small_or_imprecise_dtypes=True)
         ident = sb.tile([P, P], F32, name="ident", tag="ident")
         make_identity(nc, ident[:])
+        ident_bf = sb.tile([P, P], BF16, name="ident_bf", tag="ident_bf")
+        make_identity(nc, ident_bf[:])
 
         zero = sb.tile([P, 1], F32, name="zero", tag="zero")
         warm = sb.tile([P, 1], F32, name="warm", tag="warm")
@@ -123,18 +126,20 @@ def tile_mla_pa_kernel(tc, x, Wq_bytes, Wq_scale, Wk, out_0, out_1):
         x_codes = sb.tile([P, SEQS * PASSES * P], U32, name="x_codes", tag="x_codes", align_bytes=64)
         x_scales = sb.tile([P, SEQS * PASSES * P], U8, name="x_scales", tag="x_scales", align_bytes=64)
         x_turned = {}
-        for m in range(SEQS):
-            words = x_raw[:, m, :].bitcast(F32)
-            for gp in range(PASSES // 2):
-                x_turned[(m, gp)] = ps.tile([P, 4, P], F32, name="x_turned", tag="bank", bufs=8)
-                for gl in range(2):
-                    g = 2 * gp + gl
-                    for u in range(2):
-                        nc.tensor.transpose(
-                            x_turned[(m, gp)][:, 2 * gl + u, :],
-                            words[:, 2 * P * g + u:2 * P * (g + 1):2],
-                            ident[:],
-                        )
+
+        def turn_x():
+            for m in range(SEQS):
+                words = x_raw[:, m, :].bitcast(F32)
+                for gp in range(PASSES // 2):
+                    x_turned[(m, gp)] = ps.tile([P, 4, P], F32, name="x_turned", tag="acc", bufs=6)
+                    for gl in range(2):
+                        g = 2 * gp + gl
+                        for u in range(2):
+                            nc.tensor.transpose(
+                                x_turned[(m, gp)][:, 2 * gl + u, :],
+                                words[:, 2 * P * g + u:2 * P * (g + 1):2],
+                                ident[:],
+                            )
 
         def copy_x():
             for m in range(SEQS):
@@ -155,8 +160,10 @@ def tile_mla_pa_kernel(tc, x, Wq_bytes, Wq_scale, Wk, out_0, out_1):
             picked = tile_ap.rearrange("p t (h f) -> p h f t", f=HEAD)[:, :, lo:hi, :]
             return picked.rearrange("p h (c i) t -> p h c t i", i=RUN)
 
-        def open_round(r):
-            q_wide[r] = sb.tile([P, PACK, CHUNK], BF16, name="q_wide", tag="q_wide", bufs=3)
+        def open_wide(r):
+            q_wide[r] = sb.tile([P, PACK, CHUNK], BF16, name="q_wide", tag="q_wide", bufs=4)
+
+        def open_rope(r):
             grouped[("r", r)] = sb.tile([P, UNIT, PACK], BF16, name="grp_r", tag="grp_r", bufs=3, align_bytes=64)
 
         def widen(r, t, on_vector):
@@ -170,18 +177,41 @@ def tile_mla_pa_kernel(tc, x, Wq_bytes, Wq_scale, Wk, out_0, out_1):
         def rope_dst(r, first):
             return grouped[("r", r)][:, first:first + HALF, :].rearrange("p (h c i) t -> p h c t i", h=CH_HEADS, i=RUN)
 
-        def widen_round(r):
-            open_round(r)
-            for t in range(PACK):
-                widen(r, t, False)
-            nc.scalar.copy(out=rope_dst(r, 0), in_=by_head(q_wide[r][:], NOPE, HEAD))
-            for kind in ("k", "q"):
-                if (kind, r) in S_NOPE:
-                    interleave_nope(kind, r, nc.scalar.copy)
+        def pass_rope(r):
+            passed[r] = ps.tile([P, HALF * PACK], BF16, name="passed", tag="passed", bufs=2)
+            heads = q_wide[r][:].rearrange("p t (h f) -> p h f t", f=HEAD)
+            for j in range(2):
+                nc.tensor.matmul(
+                    out=passed[r][:, j * UNIT:(j + 1) * UNIT].rearrange("p (h f t) -> p h f t", h=2, t=PACK),
+                    lhsT=ident_bf[:],
+                    rhs=heads[:, 2 * j:2 * j + 2, NOPE:HEAD, :],
+                    start=True,
+                    stop=True,
+                )
 
-        def interleave_nope(kind, r, copy):
+        def collect_rope(r):
+            open_rope(r)
+            nc.scalar.copy(
+                out=grouped[("r", r)][:, 0:HALF, :].rearrange("p c t -> p (c t)"),
+                in_=passed[r][:],
+            )
+
+        def stage(s):
+            if s < ROUNDS:
+                open_wide(s)
+                widen(s, 0, False)
+            if 2 <= s <= ROUNDS:
+                collect_rope(s - 1)
+            if s < ROUNDS:
+                for t in range(1, PACK):
+                    widen(s, t, False)
+                for kind in ("k", "q"):
+                    if (kind, s) in S_NOPE:
+                        interleave_nope(kind, s, nc.scalar.copy, "grp_s")
+
+        def interleave_nope(kind, r, copy, tag):
             src = k_raw[r] if kind == "k" else q_wide[r]
-            grouped[(kind, r)] = sb.tile([P, UNIT, PACK], BF16, name="grp_" + kind, tag="grp_" + kind, bufs=3, align_bytes=64)
+            grouped[(kind, r)] = sb.tile([P, UNIT, PACK], BF16, name=tag, tag=tag, bufs=4, align_bytes=64)
             copy(
                 out=grouped[(kind, r)][:].rearrange("p (h c i) t -> p h c t i", h=CH_HEADS, i=RUN),
                 in_=by_head(src[:], 0, NOPE),
@@ -203,7 +233,7 @@ def tile_mla_pa_kernel(tc, x, Wq_bytes, Wq_scale, Wk, out_0, out_1):
             cd, sl = codes[(kind, r)]
             for m in range(SEQS):
                 if g == 0:
-                    acc[(kind, m)] = ps.tile([P, UNIT], F32, name="acc", tag="bank", bufs=8)
+                    acc[(kind, m)] = ps.tile([P, UNIT], F32, name="acc", tag="acc", bufs=6)
                 xcols = slice((m * PASSES + g) * P, (m * PASSES + g + 1) * P)
                 nc.tensor.matmul_mx(
                     out=acc[(kind, m)][:],
@@ -253,11 +283,15 @@ def tile_mla_pa_kernel(tc, x, Wq_bytes, Wq_scale, Wk, out_0, out_1):
                     in_=res[m][:, wi * CH_HEADS:(wi + 1) * CH_HEADS, :].rearrange("p h f -> p (h f)"),
                 )
 
-        open_round(0)
+        open_wide(0)
+        open_rope(0)
         widen(0, 0, False)
         widen(0, 1, False)
         widen(0, 2, True)
         widen(0, 3, True)
+        stage(1)
+        pass_rope(1)
+        turn_x()
 
         for r in range(ROUNDS + 1):
             closed = r > 0 and r % PASSES == 0
@@ -269,8 +303,7 @@ def tile_mla_pa_kernel(tc, x, Wq_bytes, Wq_scale, Wk, out_0, out_1):
             if closed:
                 for m in range(SEQS):
                     copy_nope("k", m)
-            if r + 1 < ROUNDS:
-                widen_round(r + 1)
+            stage(r + 2)
             if r == X_ROUND - 1:
                 copy_x()
             if r < ROUNDS:
@@ -290,7 +323,7 @@ def tile_mla_pa_kernel(tc, x, Wq_bytes, Wq_scale, Wk, out_0, out_1):
                     store(r // PASSES - 1, m)
             if r < ROUNDS:
                 if ("k", r) not in S_NOPE:
-                    interleave_nope("k", r, nc.vector.tensor_copy)
+                    interleave_nope("k", r, nc.vector.tensor_copy, "grp_k")
                 if r == 0:
                     finish_tables()
                     nc.vector.tensor_copy(out=rope_dst(0, 0), in_=by_head(q_wide[0][:], NOPE, HEAD))
@@ -298,7 +331,9 @@ def tile_mla_pa_kernel(tc, x, Wq_bytes, Wq_scale, Wk, out_0, out_1):
                 if r >= X_ROUND:
                     flush_products()
                 if ("q", r) not in S_NOPE:
-                    interleave_nope("q", r, nc.vector.tensor_copy)
+                    interleave_nope("q", r, nc.vector.tensor_copy, "grp_q")
                 quantize("k", r)
                 if r >= X_ROUND:
                     flush_products()
+                if r + 2 < ROUNDS:
+                    pass_rope(r + 2)

@@ -35,7 +35,8 @@ RUN = 4
 X_ROUND = 2
 CODE_BUFS = 10
 RATIO = 10000.0 ** (-2.0 / ROPE)
-S_NOPE = (("q", 4), ("q", 8), ("q", 10), ("q", 12), ("q", 14), ("q", 15), ("k", 15))
+S_NOPE = (("k", 3), ("k", 15))
+V_ROPE_Q = (0, 2)
 
 
 def tile_mla_pa_kernel(tc, x, Wq_bytes, Wq_scale, Wk, out_0, out_1):
@@ -60,7 +61,6 @@ def tile_mla_pa_kernel(tc, x, Wq_bytes, Wq_scale, Wk, out_0, out_1):
         acc = {}
         res = {}
         products = []
-        passed = {}
 
         def load(r):
             c, g = divmod(r, PASSES)
@@ -84,8 +84,6 @@ def tile_mla_pa_kernel(tc, x, Wq_bytes, Wq_scale, Wk, out_0, out_1):
         nc.gpsimd.iota(pos[:], pattern=[[0, 1]], base=0, channel_multiplier=1, allow_small_or_imprecise_dtypes=True)
         ident = sb.tile([P, P], F32, name="ident", tag="ident")
         make_identity(nc, ident[:])
-        ident_bf = sb.tile([P, P], BF16, name="ident_bf", tag="ident_bf")
-        make_identity(nc, ident_bf[:])
 
         zero = sb.tile([P, 1], F32, name="zero", tag="zero")
         warm = sb.tile([P, 1], F32, name="warm", tag="warm")
@@ -126,20 +124,18 @@ def tile_mla_pa_kernel(tc, x, Wq_bytes, Wq_scale, Wk, out_0, out_1):
         x_codes = sb.tile([P, SEQS * PASSES * P], U32, name="x_codes", tag="x_codes", align_bytes=64)
         x_scales = sb.tile([P, SEQS * PASSES * P], U8, name="x_scales", tag="x_scales", align_bytes=64)
         x_turned = {}
-
-        def turn_x():
-            for m in range(SEQS):
-                words = x_raw[:, m, :].bitcast(F32)
-                for gp in range(PASSES // 2):
-                    x_turned[(m, gp)] = ps.tile([P, 4, P], F32, name="x_turned", tag="acc", bufs=6)
-                    for gl in range(2):
-                        g = 2 * gp + gl
-                        for u in range(2):
-                            nc.tensor.transpose(
-                                x_turned[(m, gp)][:, 2 * gl + u, :],
-                                words[:, 2 * P * g + u:2 * P * (g + 1):2],
-                                ident[:],
-                            )
+        for m in range(SEQS):
+            words = x_raw[:, m, :].bitcast(F32)
+            for gp in range(PASSES // 2):
+                x_turned[(m, gp)] = ps.tile([P, 4, P], F32, name="x_turned", tag="bank", bufs=8)
+                for gl in range(2):
+                    g = 2 * gp + gl
+                    for u in range(2):
+                        nc.tensor.transpose(
+                            x_turned[(m, gp)][:, 2 * gl + u, :],
+                            words[:, 2 * P * g + u:2 * P * (g + 1):2],
+                            ident[:],
+                        )
 
         def copy_x():
             for m in range(SEQS):
@@ -160,10 +156,8 @@ def tile_mla_pa_kernel(tc, x, Wq_bytes, Wq_scale, Wk, out_0, out_1):
             picked = tile_ap.rearrange("p t (h f) -> p h f t", f=HEAD)[:, :, lo:hi, :]
             return picked.rearrange("p h (c i) t -> p h c t i", i=RUN)
 
-        def open_wide(r):
-            q_wide[r] = sb.tile([P, PACK, CHUNK], BF16, name="q_wide", tag="q_wide", bufs=4)
-
-        def open_rope(r):
+        def open_round(r):
+            q_wide[r] = sb.tile([P, PACK, CHUNK], BF16, name="q_wide", tag="q_wide", bufs=3)
             grouped[("r", r)] = sb.tile([P, UNIT, PACK], BF16, name="grp_r", tag="grp_r", bufs=3, align_bytes=64)
 
         def widen(r, t, on_vector):
@@ -177,41 +171,19 @@ def tile_mla_pa_kernel(tc, x, Wq_bytes, Wq_scale, Wk, out_0, out_1):
         def rope_dst(r, first):
             return grouped[("r", r)][:, first:first + HALF, :].rearrange("p (h c i) t -> p h c t i", h=CH_HEADS, i=RUN)
 
-        def pass_rope(r):
-            passed[r] = ps.tile([P, HALF * PACK], BF16, name="passed", tag="passed", bufs=2)
-            heads = q_wide[r][:].rearrange("p t (h f) -> p h f t", f=HEAD)
-            for j in range(2):
-                nc.tensor.matmul(
-                    out=passed[r][:, j * UNIT:(j + 1) * UNIT].rearrange("p (h f t) -> p h f t", h=2, t=PACK),
-                    lhsT=ident_bf[:],
-                    rhs=heads[:, 2 * j:2 * j + 2, NOPE:HEAD, :],
-                    start=True,
-                    stop=True,
-                )
+        def widen_round(r):
+            open_round(r)
+            for t in range(PACK):
+                widen(r, t, False)
+            if r not in V_ROPE_Q:
+                nc.scalar.copy(out=rope_dst(r, 0), in_=by_head(q_wide[r][:], NOPE, HEAD))
+            for kind in ("k", "q"):
+                if (kind, r) in S_NOPE:
+                    interleave_nope(kind, r, nc.scalar.copy)
 
-        def collect_rope(r):
-            open_rope(r)
-            nc.scalar.copy(
-                out=grouped[("r", r)][:, 0:HALF, :].rearrange("p c t -> p (c t)"),
-                in_=passed[r][:],
-            )
-
-        def stage(s):
-            if s < ROUNDS:
-                open_wide(s)
-                widen(s, 0, False)
-            if 2 <= s <= ROUNDS:
-                collect_rope(s - 1)
-            if s < ROUNDS:
-                for t in range(1, PACK):
-                    widen(s, t, False)
-                for kind in ("k", "q"):
-                    if (kind, s) in S_NOPE:
-                        interleave_nope(kind, s, nc.scalar.copy, "grp_s")
-
-        def interleave_nope(kind, r, copy, tag):
+        def interleave_nope(kind, r, copy):
             src = k_raw[r] if kind == "k" else q_wide[r]
-            grouped[(kind, r)] = sb.tile([P, UNIT, PACK], BF16, name=tag, tag=tag, bufs=4, align_bytes=64)
+            grouped[(kind, r)] = sb.tile([P, UNIT, PACK], BF16, name="grp_" + kind, tag="grp_" + kind, bufs=3, align_bytes=64)
             copy(
                 out=grouped[(kind, r)][:].rearrange("p (h c i) t -> p h c t i", h=CH_HEADS, i=RUN),
                 in_=by_head(src[:], 0, NOPE),
@@ -233,7 +205,7 @@ def tile_mla_pa_kernel(tc, x, Wq_bytes, Wq_scale, Wk, out_0, out_1):
             cd, sl = codes[(kind, r)]
             for m in range(SEQS):
                 if g == 0:
-                    acc[(kind, m)] = ps.tile([P, UNIT], F32, name="acc", tag="acc", bufs=6)
+                    acc[(kind, m)] = ps.tile([P, UNIT], F32, name="acc", tag="bank", bufs=8)
                 xcols = slice((m * PASSES + g) * P, (m * PASSES + g + 1) * P)
                 nc.tensor.matmul_mx(
                     out=acc[(kind, m)][:],
@@ -283,15 +255,11 @@ def tile_mla_pa_kernel(tc, x, Wq_bytes, Wq_scale, Wk, out_0, out_1):
                     in_=res[m][:, wi * CH_HEADS:(wi + 1) * CH_HEADS, :].rearrange("p h f -> p (h f)"),
                 )
 
-        open_wide(0)
-        open_rope(0)
+        open_round(0)
         widen(0, 0, False)
         widen(0, 1, False)
         widen(0, 2, True)
         widen(0, 3, True)
-        stage(1)
-        pass_rope(1)
-        turn_x()
 
         for r in range(ROUNDS + 1):
             closed = r > 0 and r % PASSES == 0
@@ -303,7 +271,8 @@ def tile_mla_pa_kernel(tc, x, Wq_bytes, Wq_scale, Wk, out_0, out_1):
             if closed:
                 for m in range(SEQS):
                     copy_nope("k", m)
-            stage(r + 2)
+            if r + 1 < ROUNDS:
+                widen_round(r + 1)
             if r == X_ROUND - 1:
                 copy_x()
             if r < ROUNDS:
@@ -323,17 +292,16 @@ def tile_mla_pa_kernel(tc, x, Wq_bytes, Wq_scale, Wk, out_0, out_1):
                     store(r // PASSES - 1, m)
             if r < ROUNDS:
                 if ("k", r) not in S_NOPE:
-                    interleave_nope("k", r, nc.vector.tensor_copy, "grp_k")
+                    interleave_nope("k", r, nc.vector.tensor_copy)
                 if r == 0:
                     finish_tables()
-                    nc.vector.tensor_copy(out=rope_dst(0, 0), in_=by_head(q_wide[0][:], NOPE, HEAD))
+                if r in V_ROPE_Q:
+                    nc.vector.tensor_copy(out=rope_dst(r, 0), in_=by_head(q_wide[r][:], NOPE, HEAD))
                 quantize("r", r)
                 if r >= X_ROUND:
                     flush_products()
                 if ("q", r) not in S_NOPE:
-                    interleave_nope("q", r, nc.vector.tensor_copy, "grp_q")
+                    interleave_nope("q", r, nc.vector.tensor_copy)
                 quantize("k", r)
                 if r >= X_ROUND:
                     flush_products()
-                if r + 2 < ROUNDS:
-                    pass_rope(r + 2)

@@ -31,7 +31,7 @@ ROUNDS = CHUNKS * PASSES
 UNIT = 512
 HALF = UNIT // 2
 AHEAD = 4
-RUN = 4
+RUN = 8
 X_ROUND = 2
 CODE_BUFS = 10
 RATIO = 10000.0 ** (-2.0 / ROPE)

@@ -60,6 +60,7 @@ def tile_mla_pa_kernel(tc, x, Wq_bytes, Wq_scale, Wk, out_0, out_1):
         codes = {}
         acc = {}
         res = {}
+        crossed = {}
         products = []
 
         def load(r):
@@ -229,31 +230,43 @@ def tile_mla_pa_kernel(tc, x, Wq_bytes, Wq_scale, Wk, out_0, out_1):
                 in_=acc[(kind, m)][:].rearrange("p (h f) -> p h f", f=NOPE),
             )
 
-        def rotate(m):
-            bank = acc[("r", m)]
-            crossed = sb.tile([P, UNIT], F32, name="crossed", tag="crossed", bufs=2)
-            nc.vector.tensor_tensor(out=crossed[:], in0=bank[:], in1=table[:, 1, :], op=ALU.mult)
+        def times_sin(m, h0, h1):
+            cols = slice(h0 * ROPE, h1 * ROPE)
+            nc.vector.tensor_tensor(out=crossed[m][:, cols], in0=acc[("r", m)][:, cols], in1=table[:, 1, cols], op=ALU.mult)
+
+        def times_cos(m, h0, h1):
+            cols = slice(h0 * ROPE, h1 * ROPE)
             nc.vector.tensor_tensor(
-                out=res[m][:, :, NOPE:HEAD],
-                in0=bank[:].rearrange("p (h f) -> p h f", f=ROPE),
-                in1=table[:, 0, :].rearrange("p (h f) -> p h f", f=ROPE),
+                out=res[m][:, h0:h1, NOPE:HEAD],
+                in0=acc[("r", m)][:, cols].rearrange("p (h f) -> p h f", f=ROPE),
+                in1=table[:, 0, cols].rearrange("p (h f) -> p h f", f=ROPE),
                 op=ALU.mult,
             )
-            pairs = res[m][:, :, NOPE:HEAD].rearrange("p h (i two) -> p h i two", two=2)
+
+        def rotate_sum(m, h0, h1):
+            pairs = res[m][:, h0:h1, NOPE:HEAD].rearrange("p h (i two) -> p h i two", two=2)
             nc.vector.tensor_tensor(
                 out=pairs,
                 in0=pairs,
-                in1=crossed[:].rearrange("p (h i two) -> p h i two", i=PAIRS, two=2)[:, :, :, ::-1],
+                in1=crossed[m][:, h0 * ROPE:h1 * ROPE].rearrange("p (h i two) -> p h i two", i=PAIRS, two=2)[:, :, :, ::-1],
                 op=ALU.add,
             )
 
-        def store(c, m):
-            cols = slice(c * CHUNK, (c + 1) * CHUNK)
-            for wi in (1, 0):
-                nc.sync.dma_start(
-                    out=outs[wi][m, :, cols],
-                    in_=res[m][:, wi * CH_HEADS:(wi + 1) * CH_HEADS, :].rearrange("p h f -> p (h f)"),
-                )
+        def rotate(parts):
+            for m in range(SEQS):
+                crossed[m] = sb.tile([P, UNIT], F32, name="crossed", tag="crossed", bufs=2)
+            for i, part in enumerate(parts):
+                times_sin(*part)
+                if i > 0:
+                    rotate_sum(*parts[i - 1])
+                times_cos(*part)
+            rotate_sum(*parts[-1])
+
+        def store(c, wi, m):
+            nc.sync.dma_start(
+                out=outs[wi][m, :, c * CHUNK:(c + 1) * CHUNK],
+                in_=res[m][:, wi * CH_HEADS:(wi + 1) * CH_HEADS, :].rearrange("p h f -> p (h f)"),
+            )
 
         open_round(0)
         widen(0, 0, False)
@@ -284,12 +297,15 @@ def tile_mla_pa_kernel(tc, x, Wq_bytes, Wq_scale, Wk, out_0, out_1):
             if r >= X_ROUND:
                 flush_products()
             if closed:
-                for m in range(SEQS):
-                    rotate(m)
+                if r < ROUNDS:
+                    rotate([(m, 0, 2 * CH_HEADS) for m in range(SEQS)])
+                else:
+                    rotate([(m, wi * CH_HEADS, (wi + 1) * CH_HEADS) for wi in (1, 0) for m in range(SEQS)])
                 for m in range(SEQS):
                     copy_nope("q", m)
-                for m in range(SEQS):
-                    store(r // PASSES - 1, m)
+                for wi in (1, 0):
+                    for m in range(SEQS):
+                        store(r // PASSES - 1, wi, m)
             if r < ROUNDS:
                 if ("k", r) not in S_NOPE:
                     interleave_nope("k", r, nc.vector.tensor_copy)

@@ -109,17 +109,13 @@ def tile_mla_pa_kernel(tc, x, Wq_bytes, Wq_scale, Wk, out_0, out_1):
         nc.vector.scalar_tensor_tensor(out=minus[:], in0=frac[:], scalar=0.5, in1=frac[:], op0=ALU.is_gt, op1=ALU.subtract)
         cos_sin = sb.tile([P, 2, PAIRS], F32, name="cos_sin", tag="cos_sin")
         nc.scalar.activation(out=cos_sin[:].rearrange("p a i -> p (a i)"), in_=minus[:], func=ACT.Sin, scale=-2.0 * math.pi)
-        table = sb.tile([P, 2, UNIT], F32, name="table", tag="table")
+        table = sb.tile([P, 2, ROPE], F32, name="table", tag="table")
 
         def finish_tables():
-            first = table[:, :, 0:ROPE].rearrange("p a (i two) -> p a i two", two=2)
+            first = table[:].rearrange("p a (i two) -> p a i two", two=2)
             nc.vector.tensor_copy(out=first[:, :, :, 0], in_=cos_sin[:])
             nc.vector.tensor_copy(out=first[:, 0, :, 1], in_=cos_sin[:, 0, :])
             nc.vector.tensor_scalar(out=first[:, 1, :, 1], in0=cos_sin[:, 1, :], scalar1=-1.0, scalar2=None, op0=ALU.mult)
-            n = ROPE
-            while n < UNIT:
-                nc.vector.tensor_copy(out=table[:, :, n:2 * n], in_=table[:, :, 0:n])
-                n *= 2
 
         x_words = sb.tile([P, SEQS, PASSES, P, 2], F32, name="x_words", tag="x_words", align_bytes=64)
         x_codes = sb.tile([P, SEQS * PASSES * P], U32, name="x_codes", tag="x_codes", align_bytes=64)
@@ -232,14 +228,19 @@ def tile_mla_pa_kernel(tc, x, Wq_bytes, Wq_scale, Wk, out_0, out_1):
 
         def times_sin(m, h0, h1):
             cols = slice(h0 * ROPE, h1 * ROPE)
-            nc.vector.tensor_tensor(out=crossed[m][:, cols], in0=acc[("r", m)][:, cols], in1=table[:, 1, cols], op=ALU.mult)
+            nc.vector.tensor_tensor(
+                out=crossed[m][:, cols].rearrange("p (h f) -> p h f", f=ROPE),
+                in0=acc[("r", m)][:, cols].rearrange("p (h f) -> p h f", f=ROPE),
+                in1=table[:, 1:2, :].to_broadcast([P, h1 - h0, ROPE]),
+                op=ALU.mult,
+            )
 
         def times_cos(m, h0, h1):
             cols = slice(h0 * ROPE, h1 * ROPE)
             nc.vector.tensor_tensor(
                 out=res[m][:, h0:h1, NOPE:HEAD],
                 in0=acc[("r", m)][:, cols].rearrange("p (h f) -> p h f", f=ROPE),
-                in1=table[:, 0, cols].rearrange("p (h f) -> p h f", f=ROPE),
+                in1=table[:, 0:1, :].to_broadcast([P, h1 - h0, ROPE]),
                 op=ALU.mult,
             )
 
@@ -257,9 +258,9 @@ def tile_mla_pa_kernel(tc, x, Wq_bytes, Wq_scale, Wk, out_0, out_1):
                 crossed[m] = sb.tile([P, UNIT], F32, name="crossed", tag="crossed", bufs=2)
             for i, part in enumerate(parts):
                 times_sin(*part)
+                times_cos(*part)
                 if i > 0:
                     rotate_sum(*parts[i - 1])
-                times_cos(*part)
             rotate_sum(*parts[-1])
 
         def store(c, wi, m):

@@ -108,7 +108,6 @@ def tile_mla_pa_kernel(tc, x, Wq_bytes, Wq_scale, Wk, out_0, out_1):
         nc.vector.tensor_tensor(out=frac[:], in0=turns_flat, in1=whole_f[:], op=ALU.subtract)
         nc.vector.scalar_tensor_tensor(out=minus[:], in0=frac[:], scalar=0.5, in1=frac[:], op0=ALU.is_gt, op1=ALU.subtract)
         cos_sin = sb.tile([P, 2, PAIRS], F32, name="cos_sin", tag="cos_sin")
-        nc.scalar.activation(out=cos_sin[:].rearrange("p a i -> p (a i)"), in_=minus[:], func=ACT.Sin, scale=-2.0 * math.pi)
         table = sb.tile([P, 2, ROPE], F32, name="table", tag="table")
 
         def finish_tables():
@@ -272,6 +271,7 @@ def tile_mla_pa_kernel(tc, x, Wq_bytes, Wq_scale, Wk, out_0, out_1):
         open_round(0)
         widen(0, 0, False)
         widen(0, 1, False)
+        nc.scalar.activation(out=cos_sin[:].rearrange("p a i -> p (a i)"), in_=minus[:], func=ACT.Sin, scale=-2.0 * math.pi)
         widen(0, 2, True)
         widen(0, 3, True)
 
@@ -291,6 +291,8 @@ def tile_mla_pa_kernel(tc, x, Wq_bytes, Wq_scale, Wk, out_0, out_1):
                 copy_x()
             if r < ROUNDS:
                 nc.vector.tensor_copy(out=rope_dst(r, HALF), in_=by_head(k_raw[r][:], NOPE, HEAD))
+            if r in V_ROPE_Q:
+                nc.vector.tensor_copy(out=rope_dst(r, 0), in_=by_head(q_wide[r][:], NOPE, HEAD))
             if r > 0:
                 quantize("q", r - 1)
             if r == X_ROUND:
@@ -312,8 +314,6 @@ def tile_mla_pa_kernel(tc, x, Wq_bytes, Wq_scale, Wk, out_0, out_1):
                     interleave_nope("k", r, nc.vector.tensor_copy)
                 if r == 0:
                     finish_tables()
-                if r in V_ROPE_Q:
-                    nc.vector.tensor_copy(out=rope_dst(r, 0), in_=by_head(q_wide[r][:], NOPE, HEAD))
                 quantize("r", r)
                 if r >= X_ROUND:
                     flush_products()

@@ -37,6 +37,7 @@ CODE_BUFS = 10
 RATIO = 10000.0 ** (-2.0 / ROPE)
 S_NOPE = (("k", 3), ("k", 15))
 V_ROPE_Q = (0, 2)
+POOL_FROM = 2
 
 
 def tile_mla_pa_kernel(tc, x, Wq_bytes, Wq_scale, Wk, out_0, out_1):
@@ -148,9 +149,12 @@ def tile_mla_pa_kernel(tc, x, Wq_bytes, Wq_scale, Wk, out_0, out_1):
                 in_=x_words[:].rearrange("p m g r u -> p (m g r u)").bitcast(BF16),
             )
 
-        def by_head(tile_ap, lo, hi):
-            picked = tile_ap.rearrange("p t (h f) -> p h f t", f=HEAD)[:, :, lo:hi, :]
+        def by_head(tile_ap, lo, hi, h0=0, h1=CH_HEADS):
+            picked = tile_ap.rearrange("p t (h f) -> p h f t", f=HEAD)[:, h0:h1, lo:hi, :]
             return picked.rearrange("p h (c i) t -> p h c t i", i=RUN)
+
+        def open_nope(kind, r):
+            grouped[(kind, r)] = sb.tile([P, UNIT, PACK], BF16, name="grp_" + kind, tag="grp_" + kind, bufs=3, align_bytes=64)
 
         def open_round(r):
             q_wide[r] = sb.tile([P, PACK, CHUNK], BF16, name="q_wide", tag="q_wide", bufs=3)
@@ -177,12 +181,26 @@ def tile_mla_pa_kernel(tc, x, Wq_bytes, Wq_scale, Wk, out_0, out_1):
                 if (kind, r) in S_NOPE:
                     interleave_nope(kind, r, nc.scalar.copy)
 
-        def interleave_nope(kind, r, copy):
+        def interleave_nope(kind, r, copy, h0=0, h1=CH_HEADS):
             src = k_raw[r] if kind == "k" else q_wide[r]
-            grouped[(kind, r)] = sb.tile([P, UNIT, PACK], BF16, name="grp_" + kind, tag="grp_" + kind, bufs=3, align_bytes=64)
+            if (kind, r) not in grouped:
+                open_nope(kind, r)
             copy(
-                out=grouped[(kind, r)][:].rearrange("p (h c i) t -> p h c t i", h=CH_HEADS, i=RUN),
-                in_=by_head(src[:], 0, NOPE),
+                out=grouped[(kind, r)][:, h0 * NOPE:h1 * NOPE, :].rearrange("p (h c i) t -> p h c t i", h=h1 - h0, i=RUN),
+                in_=by_head(src[:], 0, NOPE, h0, h1),
+            )
+
+        def pool_share(r):
+            token = sb.tile([P, 1], F32, name="token", tag="token", bufs=2)
+            nc.vector.memset(token[:], 1.0)
+            open_nope("k", r)
+            nc.gpsimd.tensor_scalar(
+                out=grouped[("k", r)][:, POOL_FROM * NOPE:UNIT, :].rearrange("p (h c) t -> p h c t", c=NOPE),
+                in0=k_raw[r][:].rearrange("p t (h f) -> p h f t", f=HEAD)[:, POOL_FROM:CH_HEADS, 0:NOPE, :],
+                scalar1=token[:, 0:1],
+                scalar2=0.0,
+                op0=ALU.mult,
+                op1=ALU.add,
             )
 
         def quantize(kind, r):
@@ -301,6 +319,7 @@ def tile_mla_pa_kernel(tc, x, Wq_bytes, Wq_scale, Wk, out_0, out_1):
                 flush_products()
             if closed:
                 if r < ROUNDS:
+                    pool_share(r)
                     rotate([(m, 0, 2 * CH_HEADS) for m in range(SEQS)])
                 else:
                     rotate([(m, wi * CH_HEADS, (wi + 1) * CH_HEADS) for wi in (1, 0) for m in range(SEQS)])
@@ -311,7 +330,7 @@ def tile_mla_pa_kernel(tc, x, Wq_bytes, Wq_scale, Wk, out_0, out_1):
                         store(r // PASSES - 1, wi, m)
             if r < ROUNDS:
                 if ("k", r) not in S_NOPE:
-                    interleave_nope("k", r, nc.vector.tensor_copy)
+                    interleave_nope("k", r, nc.vector.tensor_copy, 0, POOL_FROM if closed else CH_HEADS)
                 if r == 0:
                     finish_tables()
                 quantize("r", r)

@@ -36,7 +36,7 @@ X_ROUND = 2
 CODE_BUFS = 10
 RATIO = 10000.0 ** (-2.0 / ROPE)
 S_NOPE = (("k", 3), ("k", 15))
-V_ROPE_Q = (0, 2)
+V_ROPE_Q = (0, 1, 2, 3, 15)
 POOL_FROM = 2
 
 

@@ -37,7 +37,7 @@ CODE_BUFS = 10
 RATIO = 10000.0 ** (-2.0 / ROPE)
 S_NOPE = (("k", 3), ("k", 15))
 V_ROPE_Q = (0, 1, 2, 3, 15)
-POOL_FROM = 2
+POOL_FROM = 1
 
 
 def tile_mla_pa_kernel(tc, x, Wq_bytes, Wq_scale, Wk, out_0, out_1):
@@ -64,23 +64,30 @@ def tile_mla_pa_kernel(tc, x, Wq_bytes, Wq_scale, Wk, out_0, out_1):
         crossed = {}
         products = []
 
-        def load(r):
+        def load_q(r):
             c, g = divmod(r, PASSES)
             cols = slice(c * CHUNK, (c + 1) * CHUNK)
             q_bytes[r] = sb.tile([P, PACK, CHUNK], U8, name="q_bytes", tag="q_bytes", bufs=AHEAD + 1)
             nc.sync.dma_start(out=q_bytes[r][:], in_=wq_rows[g][:, :, cols])
+
+        def load_k(r):
+            c, g = divmod(r, PASSES)
+            cols = slice(c * CHUNK, (c + 1) * CHUNK)
             k_raw[r] = sb.tile([P, PACK, CHUNK], BF16, name="k_raw", tag="k_raw", bufs=AHEAD + 1)
             nc.sync.dma_start(out=k_raw[r][:], in_=wk_rows[g][:, :, cols])
 
         q_scale = sb.tile([P, PASSES, PACK], F32, name="q_scale", tag="q_scale")
         nc.sync.dma_start(out=q_scale[:], in_=Wq_scale.rearrange("(g p t) o -> p g (t o)", p=P, t=PACK))
-        load(0)
-        load(1)
+        for r in range(2):
+            load_q(r)
+            load_k(r)
+        load_q(2)
         x_raw = sb.tile([P, SEQS, PASSES * P * PACK], BF16, name="x_raw", tag="x_raw")
         for m in range(SEQS):
             nc.sync.dma_start(out=x_raw[:, m, :], in_=x[m])
-        load(2)
-        load(3)
+        load_k(2)
+        load_q(3)
+        load_k(3)
 
         pos = sb.tile([P, 1], F32, name="pos", tag="pos")
         nc.gpsimd.iota(pos[:], pattern=[[0, 1]], base=0, channel_multiplier=1, allow_small_or_imprecise_dtypes=True)
@@ -261,24 +268,24 @@ def tile_mla_pa_kernel(tc, x, Wq_bytes, Wq_scale, Wk, out_0, out_1):
                 op=ALU.mult,
             )
 
-        def rotate_sum(m, h0, h1):
+        def rotate_sum(engine, m, h0, h1):
             pairs = res[m][:, h0:h1, NOPE:HEAD].rearrange("p h (i two) -> p h i two", two=2)
-            nc.vector.tensor_tensor(
+            engine.tensor_tensor(
                 out=pairs,
                 in0=pairs,
                 in1=crossed[m][:, h0 * ROPE:h1 * ROPE].rearrange("p (h i two) -> p h i two", i=PAIRS, two=2)[:, :, :, ::-1],
                 op=ALU.add,
             )
 
-        def rotate(parts):
+        def rotate(parts, helper):
             for m in range(SEQS):
                 crossed[m] = sb.tile([P, UNIT], F32, name="crossed", tag="crossed", bufs=2)
             for i, part in enumerate(parts):
                 times_sin(*part)
                 times_cos(*part)
                 if i > 0:
-                    rotate_sum(*parts[i - 1])
-            rotate_sum(*parts[-1])
+                    rotate_sum(helper, *parts[i - 1])
+            rotate_sum(nc.vector, *parts[-1])
 
         def store(c, wi, m):
             nc.sync.dma_start(
@@ -299,7 +306,8 @@ def tile_mla_pa_kernel(tc, x, Wq_bytes, Wq_scale, Wk, out_0, out_1):
                 for m in range(SEQS):
                     res[m] = sb.tile([P, 2 * CH_HEADS, HEAD], F32, name="res", tag="res", bufs=4)
             if r + AHEAD < ROUNDS:
-                load(r + AHEAD)
+                load_q(r + AHEAD)
+                load_k(r + AHEAD)
             if closed:
                 for m in range(SEQS):
                     copy_nope("k", m)
@@ -320,9 +328,9 @@ def tile_mla_pa_kernel(tc, x, Wq_bytes, Wq_scale, Wk, out_0, out_1):
             if closed:
                 if r < ROUNDS:
                     pool_share(r)
-                    rotate([(m, 0, 2 * CH_HEADS) for m in range(SEQS)])
+                    rotate([(m, 0, 2 * CH_HEADS) for m in range(SEQS)], nc.vector)
                 else:
-                    rotate([(m, wi * CH_HEADS, (wi + 1) * CH_HEADS) for wi in (1, 0) for m in range(SEQS)])
+                    rotate([(m, wi * CH_HEADS, (wi + 1) * CH_HEADS) for wi in (1, 0) for m in range(SEQS)], nc.gpsimd)
                 for m in range(SEQS):
                     copy_nope("q", m)
                 for wi in (1, 0):

@@ -26,6 +26,7 @@ HEAD = NOPE + ROPE
 PAIRS = ROPE // 2
 CH_HEADS = 4
 CHUNK = CH_HEADS * HEAD
+PITCH = CHUNK + 16
 CHUNKS = 4
 ROUNDS = CHUNKS * PASSES
 UNIT = 512
@@ -73,8 +74,8 @@ def tile_mla_pa_kernel(tc, x, Wq_bytes, Wq_scale, Wk, out_0, out_1):
         def load_k(r):
             c, g = divmod(r, PASSES)
             cols = slice(c * CHUNK, (c + 1) * CHUNK)
-            k_raw[r] = sb.tile([P, PACK, CHUNK], BF16, name="k_raw", tag="k_raw", bufs=AHEAD + 1)
-            nc.sync.dma_start(out=k_raw[r][:], in_=wk_rows[g][:, :, cols])
+            k_raw[r] = sb.tile([P, PACK, PITCH], BF16, name="k_raw", tag="k_raw", bufs=AHEAD + 1)
+            nc.sync.dma_start(out=k_raw[r][:, :, 0:CHUNK], in_=wk_rows[g][:, :, cols])
 
         q_scale = sb.tile([P, PASSES, PACK], F32, name="q_scale", tag="q_scale")
         nc.sync.dma_start(out=q_scale[:], in_=Wq_scale.rearrange("(g p t) o -> p g (t o)", p=P, t=PACK))
@@ -157,23 +158,23 @@ def tile_mla_pa_kernel(tc, x, Wq_bytes, Wq_scale, Wk, out_0, out_1):
             )
 
         def by_head(tile_ap, lo, hi, h0=0, h1=CH_HEADS):
-            picked = tile_ap.rearrange("p t (h f) -> p h f t", f=HEAD)[:, h0:h1, lo:hi, :]
+            picked = tile_ap[:, :, 0:CHUNK].rearrange("p t (h f) -> p h f t", f=HEAD)[:, h0:h1, lo:hi, :]
             return picked.rearrange("p h (c i) t -> p h c t i", i=RUN)
 
         def open_nope(kind, r):
             grouped[(kind, r)] = sb.tile([P, UNIT, PACK], BF16, name="grp_" + kind, tag="grp_" + kind, bufs=3, align_bytes=64)
 
         def open_round(r):
-            q_wide[r] = sb.tile([P, PACK, CHUNK], BF16, name="q_wide", tag="q_wide", bufs=3)
+            q_wide[r] = sb.tile([P, PACK, PITCH], BF16, name="q_wide", tag="q_wide", bufs=3)
             grouped[("r", r)] = sb.tile([P, UNIT, PACK], BF16, name="grp_r", tag="grp_r", bufs=3, align_bytes=64)
 
         def widen(r, t, on_vector):
             g = r % PASSES
             src = q_bytes[r][:, t, :].bitcast(FP8)
             if on_vector:
-                nc.vector.tensor_scalar(out=q_wide[r][:, t, :], in0=src, scalar1=q_scale[:, g, t:t + 1], scalar2=None, op0=ALU.mult)
+                nc.vector.tensor_scalar(out=q_wide[r][:, t, 0:CHUNK], in0=src, scalar1=q_scale[:, g, t:t + 1], scalar2=None, op0=ALU.mult)
             else:
-                nc.scalar.activation(out=q_wide[r][:, t, :], in_=src, func=ACT.Copy, scale=q_scale[:, g, t:t + 1])
+                nc.scalar.activation(out=q_wide[r][:, t, 0:CHUNK], in_=src, func=ACT.Copy, scale=q_scale[:, g, t:t + 1])
 
         def rope_dst(r, first):
             return grouped[("r", r)][:, first:first + HALF, :].rearrange("p (h c i) t -> p h c t i", h=CH_HEADS, i=RUN)
@@ -203,7 +204,7 @@ def tile_mla_pa_kernel(tc, x, Wq_bytes, Wq_scale, Wk, out_0, out_1):
             open_nope("k", r)
             nc.gpsimd.tensor_scalar(
                 out=grouped[("k", r)][:, POOL_FROM * NOPE:UNIT, :].rearrange("p (h c) t -> p h c t", c=NOPE),
-                in0=k_raw[r][:].rearrange("p t (h f) -> p h f t", f=HEAD)[:, POOL_FROM:CH_HEADS, 0:NOPE, :],
+                in0=k_raw[r][:, :, 0:CHUNK].rearrange("p t (h f) -> p h f t", f=HEAD)[:, POOL_FROM:CH_HEADS, 0:NOPE, :],
                 scalar1=token[:, 0:1],
                 scalar2=0.0,
                 op0=ALU.mult,

@@ -36,8 +36,9 @@ RUN = 8
 X_ROUND = 2
 CODE_BUFS = 10
 RATIO = 10000.0 ** (-2.0 / ROPE)
-S_NOPE = (("k", 3), ("k", 15))
-V_ROPE_Q = (0, 1, 2, 3, 15)
+S_NOPE = (("k", 3), ("k", 9), ("k", 15))
+PE_FROM = 6
+PE_NOPE = (14,)
 POOL_FROM = 1
 
 
@@ -64,6 +65,7 @@ def tile_mla_pa_kernel(tc, x, Wq_bytes, Wq_scale, Wk, out_0, out_1):
         res = {}
         crossed = {}
         products = []
+        turned = {}
 
         def load_q(r):
             c, g = divmod(r, PASSES)
@@ -94,6 +96,8 @@ def tile_mla_pa_kernel(tc, x, Wq_bytes, Wq_scale, Wk, out_0, out_1):
         nc.gpsimd.iota(pos[:], pattern=[[0, 1]], base=0, channel_multiplier=1, allow_small_or_imprecise_dtypes=True)
         ident = sb.tile([P, P], F32, name="ident", tag="ident")
         make_identity(nc, ident[:])
+        ident_bf = sb.tile([P, P], BF16, name="ident_bf", tag="ident_bf")
+        make_identity(nc, ident_bf[:])
 
         zero = sb.tile([P, 1], F32, name="zero", tag="zero")
         warm = sb.tile([P, 1], F32, name="warm", tag="warm")
@@ -132,7 +136,7 @@ def tile_mla_pa_kernel(tc, x, Wq_bytes, Wq_scale, Wk, out_0, out_1):
         for m in range(SEQS):
             words = x_raw[:, m, :].bitcast(F32)
             for gp in range(PASSES // 2):
-                x_turned[(m, gp)] = ps.tile([P, 4, P], F32, name="x_turned", tag="bank", bufs=8)
+                x_turned[(m, gp)] = ps.tile([P, 4, P], F32, name="x_turned", tag="bank", bufs=6)
                 for gl in range(2):
                     g = 2 * gp + gl
                     for u in range(2):
@@ -180,14 +184,39 @@ def tile_mla_pa_kernel(tc, x, Wq_bytes, Wq_scale, Wk, out_0, out_1):
             return grouped[("r", r)][:, first:first + HALF, :].rearrange("p (h c i) t -> p h c t i", h=CH_HEADS, i=RUN)
 
         def widen_round(r):
-            open_round(r)
             for t in range(PACK):
                 widen(r, t, False)
-            if r not in V_ROPE_Q:
-                nc.scalar.copy(out=rope_dst(r, 0), in_=by_head(q_wide[r][:], NOPE, HEAD))
             for kind in ("k", "q"):
                 if (kind, r) in S_NOPE:
                     interleave_nope(kind, r, nc.scalar.copy)
+
+        def turn(r, part):
+            bank = ps.tile([P, UNIT * 2], BF16, name="turned", tag="turned", bufs=2)
+            turned[(r, part)] = bank
+            rows = k_raw[r][:, :, 0:CHUNK].rearrange("p t (h f) -> p h t f", f=HEAD)
+            for half in range(2):
+                if part == 0:
+                    moving = rows[:, 2 * half:2 * half + 2, :, NOPE:HEAD]
+                else:
+                    h = 2 * (part - 1) + half
+                    moving = rows[:, h:h + 1, :, 0:NOPE]
+                dst = bank[:, half * UNIT:(half + 1) * UNIT]
+                nc.tensor.matmul(
+                    out=dst.rearrange("p (h f t) -> p h t f", t=PACK, f=moving.shape[3]),
+                    lhsT=ident_bf[:],
+                    rhs=moving,
+                    start=True,
+                    stop=True,
+                )
+
+        def fetch(r, part):
+            if part == 0:
+                dst = grouped[("r", r)][:, HALF:UNIT, :]
+            else:
+                if ("k", r) not in grouped:
+                    open_nope("k", r)
+                dst = grouped[("k", r)][:, (part - 1) * HALF:part * HALF, :]
+            nc.scalar.copy(out=dst.rearrange("p c t -> p (c t)").bitcast(F32), in_=turned[(r, part)][:].bitcast(F32))
 
         def interleave_nope(kind, r, copy, h0=0, h1=CH_HEADS):
             src = k_raw[r] if kind == "k" else q_wide[r]
@@ -201,7 +230,6 @@ def tile_mla_pa_kernel(tc, x, Wq_bytes, Wq_scale, Wk, out_0, out_1):
         def pool_share(r):
             token = sb.tile([P, 1], F32, name="token", tag="token", bufs=2)
             nc.vector.memset(token[:], 1.0)
-            open_nope("k", r)
             nc.gpsimd.tensor_scalar(
                 out=grouped[("k", r)][:, POOL_FROM * NOPE:UNIT, :].rearrange("p (h c) t -> p h c t", c=NOPE),
                 in0=k_raw[r][:, :, 0:CHUNK].rearrange("p t (h f) -> p h f t", f=HEAD)[:, POOL_FROM:CH_HEADS, 0:NOPE, :],
@@ -227,7 +255,7 @@ def tile_mla_pa_kernel(tc, x, Wq_bytes, Wq_scale, Wk, out_0, out_1):
             cd, sl = codes[(kind, r)]
             for m in range(SEQS):
                 if g == 0:
-                    acc[(kind, m)] = ps.tile([P, UNIT], F32, name="acc", tag="bank", bufs=8)
+                    acc[(kind, m)] = ps.tile([P, UNIT], F32, name="acc", tag="bank", bufs=6)
                 xcols = slice((m * PASSES + g) * P, (m * PASSES + g + 1) * P)
                 nc.tensor.matmul_mx(
                     out=acc[(kind, m)][:],
@@ -309,23 +337,37 @@ def tile_mla_pa_kernel(tc, x, Wq_bytes, Wq_scale, Wk, out_0, out_1):
             if r + AHEAD < ROUNDS:
                 load_q(r + AHEAD)
                 load_k(r + AHEAD)
+            if r + 1 < ROUNDS:
+                open_round(r + 1)
+                widen_round(r + 1)
+                if r + 1 >= PE_FROM:
+                    fetch(r + 1, 0)
+                if r + 1 in PE_NOPE:
+                    turn(r + 1, 2)
+                    fetch(r + 1, 1)
+                    fetch(r + 1, 2)
             if closed:
                 for m in range(SEQS):
                     copy_nope("k", m)
-            if r + 1 < ROUNDS:
-                widen_round(r + 1)
             if r == X_ROUND - 1:
                 copy_x()
-            if r < ROUNDS:
-                nc.vector.tensor_copy(out=rope_dst(r, HALF), in_=by_head(k_raw[r][:], NOPE, HEAD))
-            if r in V_ROPE_Q:
-                nc.vector.tensor_copy(out=rope_dst(r, 0), in_=by_head(q_wide[r][:], NOPE, HEAD))
+            v_nope = r < ROUNDS and ("k", r) not in S_NOPE and r not in PE_NOPE
+            if v_nope:
+                interleave_nope("k", r, nc.vector.tensor_copy, 0, POOL_FROM if closed else CH_HEADS)
             if r > 0:
                 quantize("q", r - 1)
             if r == X_ROUND:
                 quantize_x()
             if r >= X_ROUND:
                 flush_products()
+            if PE_FROM <= r + 2 < ROUNDS:
+                turn(r + 2, 0)
+            if r + 2 in PE_NOPE:
+                turn(r + 2, 1)
+            if r < ROUNDS:
+                nc.vector.tensor_copy(out=rope_dst(r, 0), in_=by_head(q_wide[r][:], NOPE, HEAD))
+                if r < PE_FROM:
+                    nc.vector.tensor_copy(out=rope_dst(r, HALF), in_=by_head(k_raw[r][:], NOPE, HEAD))
             if closed:
                 if r < ROUNDS:
                     pool_share(r)
@@ -338,15 +380,17 @@ def tile_mla_pa_kernel(tc, x, Wq_bytes, Wq_scale, Wk, out_0, out_1):
                     for m in range(SEQS):
                         store(r // PASSES - 1, wi, m)
             if r < ROUNDS:
-                if ("k", r) not in S_NOPE:
-                    interleave_nope("k", r, nc.vector.tensor_copy, 0, POOL_FROM if closed else CH_HEADS)
+                if v_nope:
+                    quantize("k", r)
+                    if r >= X_ROUND:
+                        flush_products()
+                interleave_nope("q", r, nc.vector.tensor_copy)
                 if r == 0:
                     finish_tables()
                 quantize("r", r)
                 if r >= X_ROUND:
                     flush_products()
-                if ("q", r) not in S_NOPE:
-                    interleave_nope("q", r, nc.vector.tensor_copy)
-                quantize("k", r)
-                if r >= X_ROUND:
-                    flush_products()
+                if not v_nope:
+                    quantize("k", r)
+                    if r >= X_ROUND:
+                        flush_products()

@@ -36,10 +36,12 @@ RUN = 8
 X_ROUND = 2
 CODE_BUFS = 10
 RATIO = 10000.0 ** (-2.0 / ROPE)
-S_NOPE = (("k", 3), ("k", 9), ("k", 15))
+S_NOPE = (3, 15)
+S_ROPE = (15,)
 PE_FROM = 6
-PE_NOPE = (14,)
+PE_NOPE = (7, 11, 14)
 POOL_FROM = 1
+TABLE_ROUND = 2
 
 
 def tile_mla_pa_kernel(tc, x, Wq_bytes, Wq_scale, Wk, out_0, out_1):
@@ -63,7 +65,7 @@ def tile_mla_pa_kernel(tc, x, Wq_bytes, Wq_scale, Wk, out_0, out_1):
         codes = {}
         acc = {}
         res = {}
-        crossed = {}
+        prods = {}
         products = []
         turned = {}
 
@@ -78,6 +80,7 @@ def tile_mla_pa_kernel(tc, x, Wq_bytes, Wq_scale, Wk, out_0, out_1):
             cols = slice(c * CHUNK, (c + 1) * CHUNK)
             k_raw[r] = sb.tile([P, PACK, PITCH], BF16, name="k_raw", tag="k_raw", bufs=AHEAD + 1)
             nc.sync.dma_start(out=k_raw[r][:, :, 0:CHUNK], in_=wk_rows[g][:, :, cols])
+
 
         q_scale = sb.tile([P, PASSES, PACK], F32, name="q_scale", tag="q_scale")
         nc.sync.dma_start(out=q_scale[:], in_=Wq_scale.rearrange("(g p t) o -> p g (t o)", p=P, t=PACK))
@@ -116,12 +119,13 @@ def tile_mla_pa_kernel(tc, x, Wq_bytes, Wq_scale, Wk, out_0, out_1):
         whole_f = sb.tile([P, 2 * PAIRS], F32, name="whole_f", tag="whole_f")
         frac = sb.tile([P, 2 * PAIRS], F32, name="frac", tag="frac")
         minus = sb.tile([P, 2 * PAIRS], F32, name="minus", tag="minus")
+        cos_sin = sb.tile([P, 2, PAIRS], F32, name="cos_sin", tag="cos_sin")
+        table = sb.tile([P, 2, ROPE], F32, name="table", tag="table")
+
         nc.vector.tensor_copy(out=whole_i[:], in_=turns_flat)
         nc.vector.tensor_copy(out=whole_f[:], in_=whole_i[:])
         nc.vector.tensor_tensor(out=frac[:], in0=turns_flat, in1=whole_f[:], op=ALU.subtract)
         nc.vector.scalar_tensor_tensor(out=minus[:], in0=frac[:], scalar=0.5, in1=frac[:], op0=ALU.is_gt, op1=ALU.subtract)
-        cos_sin = sb.tile([P, 2, PAIRS], F32, name="cos_sin", tag="cos_sin")
-        table = sb.tile([P, 2, ROPE], F32, name="table", tag="table")
 
         def finish_tables():
             first = table[:].rearrange("p a (i two) -> p a i two", two=2)
@@ -166,7 +170,7 @@ def tile_mla_pa_kernel(tc, x, Wq_bytes, Wq_scale, Wk, out_0, out_1):
             return picked.rearrange("p h (c i) t -> p h c t i", i=RUN)
 
         def open_nope(kind, r):
-            grouped[(kind, r)] = sb.tile([P, UNIT, PACK], BF16, name="grp_" + kind, tag="grp_" + kind, bufs=3, align_bytes=64)
+            grouped[(kind, r)] = sb.tile([P, UNIT, PACK], BF16, name="grp_" + kind, tag="grp_" + kind, bufs=4, align_bytes=64)
 
         def open_round(r):
             q_wide[r] = sb.tile([P, PACK, PITCH], BF16, name="q_wide", tag="q_wide", bufs=3)
@@ -186,9 +190,12 @@ def tile_mla_pa_kernel(tc, x, Wq_bytes, Wq_scale, Wk, out_0, out_1):
         def widen_round(r):
             for t in range(PACK):
                 widen(r, t, False)
-            for kind in ("k", "q"):
-                if (kind, r) in S_NOPE:
-                    interleave_nope(kind, r, nc.scalar.copy)
+
+        def strided_round(r):
+            if r in S_ROPE:
+                nc.scalar.copy(out=rope_dst(r, 0), in_=by_head(q_wide[r][:], NOPE, HEAD))
+            if r in S_NOPE:
+                interleave_nope("k", r, nc.scalar.copy)
 
         def turn(r, part):
             bank = ps.tile([P, UNIT * 2], BF16, name="turned", tag="turned", bufs=2)
@@ -279,42 +286,33 @@ def tile_mla_pa_kernel(tc, x, Wq_bytes, Wq_scale, Wk, out_0, out_1):
                 in_=acc[(kind, m)][:].rearrange("p (h f) -> p h f", f=NOPE),
             )
 
-        def times_sin(m, h0, h1):
+        def times_table(m, h0, h1):
             cols = slice(h0 * ROPE, h1 * ROPE)
             nc.vector.tensor_tensor(
-                out=crossed[m][:, cols].rearrange("p (h f) -> p h f", f=ROPE),
-                in0=acc[("r", m)][:, cols].rearrange("p (h f) -> p h f", f=ROPE),
-                in1=table[:, 1:2, :].to_broadcast([P, h1 - h0, ROPE]),
-                op=ALU.mult,
-            )
-
-        def times_cos(m, h0, h1):
-            cols = slice(h0 * ROPE, h1 * ROPE)
-            nc.vector.tensor_tensor(
-                out=res[m][:, h0:h1, NOPE:HEAD],
-                in0=acc[("r", m)][:, cols].rearrange("p (h f) -> p h f", f=ROPE),
-                in1=table[:, 0:1, :].to_broadcast([P, h1 - h0, ROPE]),
+                out=prods[m][:, :, cols].rearrange("p a (h f) -> p a h f", f=ROPE),
+                in0=acc[("r", m)][:, cols].rearrange("p (h f) -> p h f", f=ROPE).unsqueeze(1).to_broadcast([P, 2, h1 - h0, ROPE]),
+                in1=table[:].unsqueeze(2).to_broadcast([P, 2, h1 - h0, ROPE]),
                 op=ALU.mult,
             )
 
         def rotate_sum(engine, m, h0, h1):
-            pairs = res[m][:, h0:h1, NOPE:HEAD].rearrange("p h (i two) -> p h i two", two=2)
+            cols = slice(h0 * ROPE, h1 * ROPE)
             engine.tensor_tensor(
-                out=pairs,
-                in0=pairs,
-                in1=crossed[m][:, h0 * ROPE:h1 * ROPE].rearrange("p (h i two) -> p h i two", i=PAIRS, two=2)[:, :, :, ::-1],
+                out=res[m][:, h0:h1, NOPE:HEAD].rearrange("p h (i two) -> p h i two", two=2),
+                in0=prods[m][:, 0, cols].rearrange("p (h i two) -> p h i two", i=PAIRS, two=2),
+                in1=prods[m][:, 1, cols].rearrange("p (h i two) -> p h i two", i=PAIRS, two=2)[:, :, :, ::-1],
                 op=ALU.add,
             )
 
-        def rotate(parts, helper):
+        def rotate(parts, on_pool):
             for m in range(SEQS):
-                crossed[m] = sb.tile([P, UNIT], F32, name="crossed", tag="crossed", bufs=2)
+                prods[m] = sb.tile([P, 2, UNIT], F32, name="prods", tag="prods", bufs=2)
             for i, part in enumerate(parts):
-                times_sin(*part)
-                times_cos(*part)
-                if i > 0:
-                    rotate_sum(helper, *parts[i - 1])
-            rotate_sum(nc.vector, *parts[-1])
+                times_table(*part)
+                if 0 < i <= on_pool:
+                    rotate_sum(nc.gpsimd, *parts[i - 1])
+            for part in parts[on_pool:]:
+                rotate_sum(nc.vector, *part)
 
         def store(c, wi, m):
             nc.sync.dma_start(
@@ -325,7 +323,6 @@ def tile_mla_pa_kernel(tc, x, Wq_bytes, Wq_scale, Wk, out_0, out_1):
         open_round(0)
         widen(0, 0, False)
         widen(0, 1, False)
-        nc.scalar.activation(out=cos_sin[:].rearrange("p a i -> p (a i)"), in_=minus[:], func=ACT.Sin, scale=-2.0 * math.pi)
         widen(0, 2, True)
         widen(0, 3, True)
 
@@ -342,16 +339,18 @@ def tile_mla_pa_kernel(tc, x, Wq_bytes, Wq_scale, Wk, out_0, out_1):
                 widen_round(r + 1)
                 if r + 1 >= PE_FROM:
                     fetch(r + 1, 0)
+                strided_round(r + 1)
+                if r + 2 in PE_NOPE:
+                    fetch(r + 2, 1)
                 if r + 1 in PE_NOPE:
-                    turn(r + 1, 2)
-                    fetch(r + 1, 1)
                     fetch(r + 1, 2)
             if closed:
                 for m in range(SEQS):
                     copy_nope("k", m)
             if r == X_ROUND - 1:
+                nc.scalar.activation(out=cos_sin[:].rearrange("p a i -> p (a i)"), in_=minus[:], func=ACT.Sin, scale=-2.0 * math.pi)
                 copy_x()
-            v_nope = r < ROUNDS and ("k", r) not in S_NOPE and r not in PE_NOPE
+            v_nope = r < ROUNDS and r not in S_NOPE and r not in PE_NOPE
             if v_nope:
                 interleave_nope("k", r, nc.vector.tensor_copy, 0, POOL_FROM if closed else CH_HEADS)
             if r > 0:
@@ -362,18 +361,17 @@ def tile_mla_pa_kernel(tc, x, Wq_bytes, Wq_scale, Wk, out_0, out_1):
                 flush_products()
             if PE_FROM <= r + 2 < ROUNDS:
                 turn(r + 2, 0)
-            if r + 2 in PE_NOPE:
-                turn(r + 2, 1)
             if r < ROUNDS:
-                nc.vector.tensor_copy(out=rope_dst(r, 0), in_=by_head(q_wide[r][:], NOPE, HEAD))
+                if r not in S_ROPE:
+                    nc.vector.tensor_copy(out=rope_dst(r, 0), in_=by_head(q_wide[r][:], NOPE, HEAD))
                 if r < PE_FROM:
                     nc.vector.tensor_copy(out=rope_dst(r, HALF), in_=by_head(k_raw[r][:], NOPE, HEAD))
             if closed:
                 if r < ROUNDS:
                     pool_share(r)
-                    rotate([(m, 0, 2 * CH_HEADS) for m in range(SEQS)], nc.vector)
+                    rotate([(m, 0, 2 * CH_HEADS) for m in range(SEQS)], 0)
                 else:
-                    rotate([(m, wi * CH_HEADS, (wi + 1) * CH_HEADS) for wi in (1, 0) for m in range(SEQS)], nc.gpsimd)
+                    rotate([(m, wi * CH_HEADS, (wi + 1) * CH_HEADS) for wi in (1, 0) for m in range(SEQS)], 2)
                 for m in range(SEQS):
                     copy_nope("q", m)
                 for wi in (1, 0):
@@ -384,8 +382,12 @@ def tile_mla_pa_kernel(tc, x, Wq_bytes, Wq_scale, Wk, out_0, out_1):
                     quantize("k", r)
                     if r >= X_ROUND:
                         flush_products()
+                if r + 3 in PE_NOPE:
+                    turn(r + 3, 1)
+                if r + 2 in PE_NOPE:
+                    turn(r + 2, 2)
                 interleave_nope("q", r, nc.vector.tensor_copy)
-                if r == 0:
+                if r == TABLE_ROUND:
                     finish_tables()
                 quantize("r", r)
                 if r >= X_ROUND:

@@ -37,9 +37,9 @@ X_ROUND = 2
 CODE_BUFS = 10
 RATIO = 10000.0 ** (-2.0 / ROPE)
 S_NOPE = (3, 15)
-S_ROPE = (15,)
-PE_FROM = 6
-PE_NOPE = (7, 11, 14)
+S_ROPE = ()
+PE_FROM = 5
+PE_NOPE = (6, 9, 11, 14)
 POOL_FROM = 1
 TABLE_ROUND = 2
 

@@ -26,7 +26,7 @@ HEAD = NOPE + ROPE
 PAIRS = ROPE // 2
 CH_HEADS = 4
 CHUNK = CH_HEADS * HEAD
-PITCH = CHUNK + 16
+PITCH = CHUNK + 128
 CHUNKS = 4
 ROUNDS = CHUNKS * PASSES
 UNIT = 512
@@ -42,6 +42,7 @@ PE_FROM = 5
 PE_NOPE = (6, 9, 11, 14)
 POOL_FROM = 1
 TABLE_ROUND = 2
+V_HEADS_LAST = 2
 
 
 def tile_mla_pa_kernel(tc, x, Wq_bytes, Wq_scale, Wk, out_0, out_1):
@@ -82,11 +83,18 @@ def tile_mla_pa_kernel(tc, x, Wq_bytes, Wq_scale, Wk, out_0, out_1):
             nc.sync.dma_start(out=k_raw[r][:, :, 0:CHUNK], in_=wk_rows[g][:, :, cols])
 
 
-        q_scale = sb.tile([P, PASSES, PACK], F32, name="q_scale", tag="q_scale")
-        nc.sync.dma_start(out=q_scale[:], in_=Wq_scale.rearrange("(g p t) o -> p g (t o)", p=P, t=PACK))
-        for r in range(2):
-            load_q(r)
-            load_k(r)
+        scale_rows = Wq_scale.rearrange("(g p t) o -> p g (t o)", p=P, t=PACK)
+        q_scale = sb.tile([P, PASSES, 2 * PACK], F32, name="q_scale", tag="q_scale")
+
+        def load_scale(g0, g1):
+            nc.sync.dma_start(out=q_scale[:, g0:g1, 0:PACK], in_=scale_rows[:, g0:g1, :])
+
+        load_scale(0, 1)
+        load_q(0)
+        load_k(0)
+        load_scale(1, PASSES)
+        load_q(1)
+        load_k(1)
         load_q(2)
         x_raw = sb.tile([P, SEQS, PASSES * P * PACK], BF16, name="x_raw", tag="x_raw")
         for m in range(SEQS):
@@ -196,6 +204,8 @@ def tile_mla_pa_kernel(tc, x, Wq_bytes, Wq_scale, Wk, out_0, out_1):
                 nc.scalar.copy(out=rope_dst(r, 0), in_=by_head(q_wide[r][:], NOPE, HEAD))
             if r in S_NOPE:
                 interleave_nope("k", r, nc.scalar.copy)
+            if r == ROUNDS - 1:
+                interleave_nope("q", r, nc.scalar.copy, V_HEADS_LAST, CH_HEADS)
 
         def turn(r, part):
             bank = ps.tile([P, UNIT * 2], BF16, name="turned", tag="turned", bufs=2)
@@ -215,6 +225,12 @@ def tile_mla_pa_kernel(tc, x, Wq_bytes, Wq_scale, Wk, out_0, out_1):
                     start=True,
                     stop=True,
                 )
+
+        def turn_plain(r):
+            if r + 3 in PE_NOPE:
+                turn(r + 3, 1)
+            if r + 2 in PE_NOPE:
+                turn(r + 2, 2)
 
         def fetch(r, part):
             if part == 0:
@@ -304,15 +320,9 @@ def tile_mla_pa_kernel(tc, x, Wq_bytes, Wq_scale, Wk, out_0, out_1):
                 op=ALU.add,
             )
 
-        def rotate(parts, on_pool):
+        def open_products():
             for m in range(SEQS):
                 prods[m] = sb.tile([P, 2, UNIT], F32, name="prods", tag="prods", bufs=2)
-            for i, part in enumerate(parts):
-                times_table(*part)
-                if 0 < i <= on_pool:
-                    rotate_sum(nc.gpsimd, *parts[i - 1])
-            for part in parts[on_pool:]:
-                rotate_sum(nc.vector, *part)
 
         def store(c, wi, m):
             nc.sync.dma_start(
@@ -353,6 +363,11 @@ def tile_mla_pa_kernel(tc, x, Wq_bytes, Wq_scale, Wk, out_0, out_1):
             v_nope = r < ROUNDS and r not in S_NOPE and r not in PE_NOPE
             if v_nope:
                 interleave_nope("k", r, nc.vector.tensor_copy, 0, POOL_FROM if closed else CH_HEADS)
+            if r == ROUNDS:
+                open_products()
+                times_table(0, CH_HEADS, 2 * CH_HEADS)
+                rotate_sum(nc.gpsimd, 0, CH_HEADS, 2 * CH_HEADS)
+                times_table(1, CH_HEADS, 2 * CH_HEADS)
             if r > 0:
                 quantize("q", r - 1)
             if r == X_ROUND:
@@ -369,9 +384,17 @@ def tile_mla_pa_kernel(tc, x, Wq_bytes, Wq_scale, Wk, out_0, out_1):
             if closed:
                 if r < ROUNDS:
                     pool_share(r)
-                    rotate([(m, 0, 2 * CH_HEADS) for m in range(SEQS)], 0)
+                    open_products()
+                    for m in range(SEQS):
+                        times_table(m, 0, 2 * CH_HEADS)
+                    for m in range(SEQS):
+                        rotate_sum(nc.vector, m, 0, 2 * CH_HEADS)
                 else:
-                    rotate([(m, wi * CH_HEADS, (wi + 1) * CH_HEADS) for wi in (1, 0) for m in range(SEQS)], 2)
+                    rotate_sum(nc.gpsimd, 1, CH_HEADS, 2 * CH_HEADS)
+                    for m in range(SEQS):
+                        times_table(m, 0, CH_HEADS)
+                    for m in range(SEQS):
+                        rotate_sum(nc.vector, m, 0, CH_HEADS)
                 for m in range(SEQS):
                     copy_nope("q", m)
                 for wi in (1, 0):
@@ -382,16 +405,17 @@ def tile_mla_pa_kernel(tc, x, Wq_bytes, Wq_scale, Wk, out_0, out_1):
                     quantize("k", r)
                     if r >= X_ROUND:
                         flush_products()
-                if r + 3 in PE_NOPE:
-                    turn(r + 3, 1)
-                if r + 2 in PE_NOPE:
-                    turn(r + 2, 2)
-                interleave_nope("q", r, nc.vector.tensor_copy)
+                closing = r % PASSES == PASSES - 1
+                if not closing:
+                    turn_plain(r)
+                interleave_nope("q", r, nc.vector.tensor_copy, 0, V_HEADS_LAST if r == ROUNDS - 1 else CH_HEADS)
                 if r == TABLE_ROUND:
                     finish_tables()
                 quantize("r", r)
                 if r >= X_ROUND:
                     flush_products()
+                if closing:
+                    turn_plain(r)
                 if not v_nope:
                     quantize("k", r)
                     if r >= X_ROUND:

from contextlib import ExitStack
import math

import concourse.mybir as mybir
from concourse.masks import make_identity

FLOPS = 2 * 256 * 2048 * 6144

F32 = mybir.dt.float32
BF16 = mybir.dt.bfloat16
I32 = mybir.dt.int32
U32 = mybir.dt.uint32
U8 = mybir.dt.uint8
FP8 = mybir.dt.float8_e4m3fn
FP8X4 = mybir.dt.float8_e4m3fn_x4
ALU = mybir.AluOpType
ACT = mybir.ActivationFunctionType

P = 128
PACK = 4
PASSES = 4
SEQS = 2
NOPE = 128
ROPE = 64
HEAD = NOPE + ROPE
PAIRS = ROPE // 2
CH_HEADS = 4
CHUNK = CH_HEADS * HEAD
PITCH = CHUNK + 128
CHUNKS = 4
ROUNDS = CHUNKS * PASSES
UNIT = 512
HALF = UNIT // 2
AHEAD = 4
RUN = 8
X_ROUND = 2
CODE_BUFS = 10
RATIO = 10000.0 ** (-2.0 / ROPE)
S_NOPE = (3, 15)
S_ROPE = ()
PE_FROM = 5
PE_NOPE = (6, 9, 11, 14)
POOL_FROM = 1
TABLE_ROUND = 2
V_HEADS_LAST = 2


def tile_mla_pa_kernel(tc, x, Wq_bytes, Wq_scale, Wk, out_0, out_1):
    nc = tc.nc
    wk_rows = Wk.rearrange("(g p t) n -> g p t n", p=P, t=PACK)
    wq_rows = Wq_bytes.rearrange("(g p t) n -> g p t n", p=P, t=PACK)
    outs = (
        out_0.rearrange("b s h f -> b s (h f)"),
        out_1.rearrange("b s h f -> b s (h f)"),
    )

    with ExitStack() as ctx:
        sb = ctx.enter_context(tc.tile_pool(name="sb", bufs=1))
        ps = ctx.enter_context(tc.psum_pool(name="ps", bufs=1))
        ctx.enter_context(tc.manual_schedule())

        q_bytes = {}
        k_raw = {}
        q_wide = {}
        grouped = {}
        codes = {}
        acc = {}
        res = {}
        prods = {}
        products = []
        turned = {}

        def load_q(r):
            c, g = divmod(r, PASSES)
            cols = slice(c * CHUNK, (c + 1) * CHUNK)
            q_bytes[r] = sb.tile([P, PACK, CHUNK], U8, name="q_bytes", tag="q_bytes", bufs=AHEAD + 1)
            nc.sync.dma_start(out=q_bytes[r][:], in_=wq_rows[g][:, :, cols])

        def load_k(r):
            c, g = divmod(r, PASSES)
            cols = slice(c * CHUNK, (c + 1) * CHUNK)
            k_raw[r] = sb.tile([P, PACK, PITCH], BF16, name="k_raw", tag="k_raw", bufs=AHEAD + 1)
            nc.sync.dma_start(out=k_raw[r][:, :, 0:CHUNK], in_=wk_rows[g][:, :, cols])


        scale_rows = Wq_scale.rearrange("(g p t) o -> p g (t o)", p=P, t=PACK)
        q_scale = sb.tile([P, PASSES, 2 * PACK], F32, name="q_scale", tag="q_scale")

        def load_scale(g0, g1):
            nc.sync.dma_start(out=q_scale[:, g0:g1, 0:PACK], in_=scale_rows[:, g0:g1, :])

        load_scale(0, 1)
        load_q(0)
        load_k(0)
        load_scale(1, PASSES)
        load_q(1)
        load_k(1)
        load_q(2)
        x_raw = sb.tile([P, SEQS, PASSES * P * PACK], BF16, name="x_raw", tag="x_raw")
        for m in range(SEQS):
            nc.sync.dma_start(out=x_raw[:, m, :], in_=x[m])
        load_k(2)
        load_q(3)
        load_k(3)

        pos = sb.tile([P, 1], F32, name="pos", tag="pos")
        nc.gpsimd.iota(pos[:], pattern=[[0, 1]], base=0, channel_multiplier=1, allow_small_or_imprecise_dtypes=True)
        ident = sb.tile([P, P], F32, name="ident", tag="ident")
        make_identity(nc, ident[:])
        ident_bf = sb.tile([P, P], BF16, name="ident_bf", tag="ident_bf")
        make_identity(nc, ident_bf[:])

        zero = sb.tile([P, 1], F32, name="zero", tag="zero")
        warm = sb.tile([P, 1], F32, name="warm", tag="warm")
        nc.vector.memset(zero[:], 0.0)
        nc.scalar.activation(out=warm[:], in_=zero[:], func=ACT.Sin)

        turns = sb.tile([P, 2, PAIRS], F32, name="turns", tag="turns")
        nc.vector.tensor_scalar(out=turns[:, 1, 0:1], in0=pos[:], scalar1=1.0 / (2.0 * math.pi), scalar2=None, op0=ALU.mult)
        w = 1
        while w < PAIRS:
            nc.vector.tensor_scalar(out=turns[:, 1, w:2 * w], in0=turns[:, 1, 0:w], scalar1=RATIO ** w, scalar2=None, op0=ALU.mult)
            w *= 2
        nc.vector.tensor_scalar(out=turns[:, 0, :], in0=turns[:, 1, :], scalar1=0.25, scalar2=None, op0=ALU.add)
        turns_flat = turns[:].rearrange("p a i -> p (a i)")
        whole_i = sb.tile([P, 2 * PAIRS], I32, name="whole_i", tag="whole_i")
        whole_f = sb.tile([P, 2 * PAIRS], F32, name="whole_f", tag="whole_f")
        frac = sb.tile([P, 2 * PAIRS], F32, name="frac", tag="frac")
        minus = sb.tile([P, 2 * PAIRS], F32, name="minus", tag="minus")
        cos_sin = sb.tile([P, 2, PAIRS], F32, name="cos_sin", tag="cos_sin")
        table = sb.tile([P, 2, ROPE], F32, name="table", tag="table")

        nc.vector.tensor_copy(out=whole_i[:], in_=turns_flat)
        nc.vector.tensor_copy(out=whole_f[:], in_=whole_i[:])
        nc.vector.tensor_tensor(out=frac[:], in0=turns_flat, in1=whole_f[:], op=ALU.subtract)
        nc.vector.scalar_tensor_tensor(out=minus[:], in0=frac[:], scalar=0.5, in1=frac[:], op0=ALU.is_gt, op1=ALU.subtract)

        def finish_tables():
            first = table[:].rearrange("p a (i two) -> p a i two", two=2)
            nc.vector.tensor_copy(out=first[:, :, :, 0], in_=cos_sin[:])
            nc.vector.tensor_copy(out=first[:, 0, :, 1], in_=cos_sin[:, 0, :])
            nc.vector.tensor_scalar(out=first[:, 1, :, 1], in0=cos_sin[:, 1, :], scalar1=-1.0, scalar2=None, op0=ALU.mult)

        x_words = sb.tile([P, SEQS, PASSES, P, 2], F32, name="x_words", tag="x_words", align_bytes=64)
        x_codes = sb.tile([P, SEQS * PASSES * P], U32, name="x_codes", tag="x_codes", align_bytes=64)
        x_scales = sb.tile([P, SEQS * PASSES * P], U8, name="x_scales", tag="x_scales", align_bytes=64)
        x_turned = {}
        for m in range(SEQS):
            words = x_raw[:, m, :].bitcast(F32)
            for gp in range(PASSES // 2):
                x_turned[(m, gp)] = ps.tile([P, 4, P], F32, name="x_turned", tag="bank", bufs=6)
                for gl in range(2):
                    g = 2 * gp + gl
                    for u in range(2):
                        nc.tensor.transpose(
                            x_turned[(m, gp)][:, 2 * gl + u, :],
                            words[:, 2 * P * g + u:2 * P * (g + 1):2],
                            ident[:],
                        )

        def copy_x():
            for m in range(SEQS):
                for gp in range(PASSES // 2):
                    nc.scalar.copy(
                        out=x_words[:, m, 2 * gp:2 * gp + 2, :, :],
                        in_=x_turned[(m, gp)][:].rearrange("p (g u) r -> p g r u", u=2),
                    )

        def quantize_x():
            nc.vector.quantize_mx(
                out=x_codes[:].bitcast(FP8X4),
                scales=x_scales[:],
                in_=x_words[:].rearrange("p m g r u -> p (m g r u)").bitcast(BF16),
            )

        def by_head(tile_ap, lo, hi, h0=0, h1=CH_HEADS):
            picked = tile_ap[:, :, 0:CHUNK].rearrange("p t (h f) -> p h f t", f=HEAD)[:, h0:h1, lo:hi, :]
            return picked.rearrange("p h (c i) t -> p h c t i", i=RUN)

        def open_nope(kind, r):
            grouped[(kind, r)] = sb.tile([P, UNIT, PACK], BF16, name="grp_" + kind, tag="grp_" + kind, bufs=4, align_bytes=64)

        def open_round(r):
            q_wide[r] = sb.tile([P, PACK, PITCH], BF16, name="q_wide", tag="q_wide", bufs=3)
            grouped[("r", r)] = sb.tile([P, UNIT, PACK], BF16, name="grp_r", tag="grp_r", bufs=3, align_bytes=64)

        def widen(r, t, on_vector):
            g = r % PASSES
            src = q_bytes[r][:, t, :].bitcast(FP8)
            if on_vector:
                nc.vector.tensor_scalar(out=q_wide[r][:, t, 0:CHUNK], in0=src, scalar1=q_scale[:, g, t:t + 1], scalar2=None, op0=ALU.mult)
            else:
                nc.scalar.activation(out=q_wide[r][:, t, 0:CHUNK], in_=src, func=ACT.Copy, scale=q_scale[:, g, t:t + 1])

        def rope_dst(r, first):
            return grouped[("r", r)][:, first:first + HALF, :].rearrange("p (h c i) t -> p h c t i", h=CH_HEADS, i=RUN)

        def widen_round(r):
            for t in range(PACK):
                widen(r, t, False)

        def strided_round(r):
            if r in S_ROPE:
                nc.scalar.copy(out=rope_dst(r, 0), in_=by_head(q_wide[r][:], NOPE, HEAD))
            if r in S_NOPE:
                interleave_nope("k", r, nc.scalar.copy)
            if r == ROUNDS - 1:
                interleave_nope("q", r, nc.scalar.copy, V_HEADS_LAST, CH_HEADS)

        def turn(r, part):
            bank = ps.tile([P, UNIT * 2], BF16, name="turned", tag="turned", bufs=2)
            turned[(r, part)] = bank
            rows = k_raw[r][:, :, 0:CHUNK].rearrange("p t (h f) -> p h t f", f=HEAD)
            for half in range(2):
                if part == 0:
                    moving = rows[:, 2 * half:2 * half + 2, :, NOPE:HEAD]
                else:
                    h = 2 * (part - 1) + half
                    moving = rows[:, h:h + 1, :, 0:NOPE]
                dst = bank[:, half * UNIT:(half + 1) * UNIT]
                nc.tensor.matmul(
                    out=dst.rearrange("p (h f t) -> p h t f", t=PACK, f=moving.shape[3]),
                    lhsT=ident_bf[:],
                    rhs=moving,
                    start=True,
                    stop=True,
                )

        def turn_plain(r):
            if r + 3 in PE_NOPE:
                turn(r + 3, 1)
            if r + 2 in PE_NOPE:
                turn(r + 2, 2)

        def fetch(r, part):
            if part == 0:
                dst = grouped[("r", r)][:, HALF:UNIT, :]
            else:
                if ("k", r) not in grouped:
                    open_nope("k", r)
                dst = grouped[("k", r)][:, (part - 1) * HALF:part * HALF, :]
            nc.scalar.copy(out=dst.rearrange("p c t -> p (c t)").bitcast(F32), in_=turned[(r, part)][:].bitcast(F32))

        def interleave_nope(kind, r, copy, h0=0, h1=CH_HEADS):
            src = k_raw[r] if kind == "k" else q_wide[r]
            if (kind, r) not in grouped:
                open_nope(kind, r)
            copy(
                out=grouped[(kind, r)][:, h0 * NOPE:h1 * NOPE, :].rearrange("p (h c i) t -> p h c t i", h=h1 - h0, i=RUN),
                in_=by_head(src[:], 0, NOPE, h0, h1),
            )

        def pool_share(r):
            token = sb.tile([P, 1], F32, name="token", tag="token", bufs=2)
            nc.vector.memset(token[:], 1.0)
            nc.gpsimd.tensor_scalar(
                out=grouped[("k", r)][:, POOL_FROM * NOPE:UNIT, :].rearrange("p (h c) t -> p h c t", c=NOPE),
                in0=k_raw[r][:, :, 0:CHUNK].rearrange("p t (h f) -> p h f t", f=HEAD)[:, POOL_FROM:CH_HEADS, 0:NOPE, :],
                scalar1=token[:, 0:1],
                scalar2=0.0,
                op0=ALU.mult,
                op1=ALU.add,
            )

        def quantize(kind, r):
            cd = sb.tile([P, UNIT], U32, name="codes", tag="codes", bufs=CODE_BUFS, align_bytes=64)
            sl = sb.tile([P, UNIT], U8, name="scales", tag="scales", bufs=CODE_BUFS, align_bytes=64)
            nc.vector.quantize_mx(
                out=cd[:].bitcast(FP8X4),
                scales=sl[:],
                in_=grouped[(kind, r)][:].rearrange("p c t -> p (c t)"),
            )
            codes[(kind, r)] = (cd, sl)
            products.append((kind, r))

        def multiply(kind, r):
            g = r % PASSES
            cd, sl = codes[(kind, r)]
            for m in range(SEQS):
                if g == 0:
                    acc[(kind, m)] = ps.tile([P, UNIT], F32, name="acc", tag="bank", bufs=6)
                xcols = slice((m * PASSES + g) * P, (m * PASSES + g + 1) * P)
                nc.tensor.matmul_mx(
                    out=acc[(kind, m)][:],
                    lhsT=x_codes[:, xcols].bitcast(FP8X4),
                    lhsT_scale=x_scales[:, xcols],
                    rhs=cd[:].bitcast(FP8X4),
                    rhs_scale=sl[:],
                    start=(g == 0),
                    stop=(g == PASSES - 1),
                )

        def flush_products():
            for kind, r in products:
                multiply(kind, r)
            products.clear()

        def copy_nope(kind, m):
            first = 0 if kind == "q" else CH_HEADS
            nc.scalar.copy(
                out=res[m][:, first:first + CH_HEADS, 0:NOPE],
                in_=acc[(kind, m)][:].rearrange("p (h f) -> p h f", f=NOPE),
            )

        def times_table(m, h0, h1):
            cols = slice(h0 * ROPE, h1 * ROPE)
            nc.vector.tensor_tensor(
                out=prods[m][:, :, cols].rearrange("p a (h f) -> p a h f", f=ROPE),
                in0=acc[("r", m)][:, cols].rearrange("p (h f) -> p h f", f=ROPE).unsqueeze(1).to_broadcast([P, 2, h1 - h0, ROPE]),
                in1=table[:].unsqueeze(2).to_broadcast([P, 2, h1 - h0, ROPE]),
                op=ALU.mult,
            )

        def rotate_sum(engine, m, h0, h1):
            cols = slice(h0 * ROPE, h1 * ROPE)
            engine.tensor_tensor(
                out=res[m][:, h0:h1, NOPE:HEAD].rearrange("p h (i two) -> p h i two", two=2),
                in0=prods[m][:, 0, cols].rearrange("p (h i two) -> p h i two", i=PAIRS, two=2),
                in1=prods[m][:, 1, cols].rearrange("p (h i two) -> p h i two", i=PAIRS, two=2)[:, :, :, ::-1],
                op=ALU.add,
            )

        def open_products():
            for m in range(SEQS):
                prods[m] = sb.tile([P, 2, UNIT], F32, name="prods", tag="prods", bufs=2)

        def store(c, wi, m):
            nc.sync.dma_start(
                out=outs[wi][m, :, c * CHUNK:(c + 1) * CHUNK],
                in_=res[m][:, wi * CH_HEADS:(wi + 1) * CH_HEADS, :].rearrange("p h f -> p (h f)"),
            )

        open_round(0)
        widen(0, 0, False)
        widen(0, 1, False)
        widen(0, 2, True)
        widen(0, 3, True)

        for r in range(ROUNDS + 1):
            closed = r > 0 and r % PASSES == 0
            if closed:
                for m in range(SEQS):
                    res[m] = sb.tile([P, 2 * CH_HEADS, HEAD], F32, name="res", tag="res", bufs=4)
            if r + AHEAD < ROUNDS:
                load_q(r + AHEAD)
                load_k(r + AHEAD)
            if r + 1 < ROUNDS:
                open_round(r + 1)
                widen_round(r + 1)
                if r + 1 >= PE_FROM:
                    fetch(r + 1, 0)
                strided_round(r + 1)
                if r + 2 in PE_NOPE:
                    fetch(r + 2, 1)
                if r + 1 in PE_NOPE:
                    fetch(r + 1, 2)
            if closed:
                for m in range(SEQS):
                    copy_nope("k", m)
            if r == X_ROUND - 1:
                nc.scalar.activation(out=cos_sin[:].rearrange("p a i -> p (a i)"), in_=minus[:], func=ACT.Sin, scale=-2.0 * math.pi)
                copy_x()
            v_nope = r < ROUNDS and r not in S_NOPE and r not in PE_NOPE
            if v_nope:
                interleave_nope("k", r, nc.vector.tensor_copy, 0, POOL_FROM if closed else CH_HEADS)
            if r == ROUNDS:
                open_products()
                times_table(0, CH_HEADS, 2 * CH_HEADS)
                rotate_sum(nc.gpsimd, 0, CH_HEADS, 2 * CH_HEADS)
                times_table(1, CH_HEADS, 2 * CH_HEADS)
            if r > 0:
                quantize("q", r - 1)
            if r == X_ROUND:
                quantize_x()
            if r >= X_ROUND:
                flush_products()
            if PE_FROM <= r + 2 < ROUNDS:
                turn(r + 2, 0)
            if r < ROUNDS:
                if r not in S_ROPE:
                    nc.vector.tensor_copy(out=rope_dst(r, 0), in_=by_head(q_wide[r][:], NOPE, HEAD))
                if r < PE_FROM:
                    nc.vector.tensor_copy(out=rope_dst(r, HALF), in_=by_head(k_raw[r][:], NOPE, HEAD))
            if closed:
                if r < ROUNDS:
                    pool_share(r)
                    open_products()
                    for m in range(SEQS):
                        times_table(m, 0, 2 * CH_HEADS)
                    for m in range(SEQS):
                        rotate_sum(nc.vector, m, 0, 2 * CH_HEADS)
                else:
                    rotate_sum(nc.gpsimd, 1, CH_HEADS, 2 * CH_HEADS)
                    for m in range(SEQS):
                        times_table(m, 0, CH_HEADS)
                    for m in range(SEQS):
                        rotate_sum(nc.vector, m, 0, CH_HEADS)
                for m in range(SEQS):
                    copy_nope("q", m)
                for wi in (1, 0):
                    for m in range(SEQS):
                        store(r // PASSES - 1, wi, m)
            if r < ROUNDS:
                if v_nope:
                    quantize("k", r)
                    if r >= X_ROUND:
                        flush_products()
                closing = r % PASSES == PASSES - 1
                if not closing:
                    turn_plain(r)
                interleave_nope("q", r, nc.vector.tensor_copy, 0, V_HEADS_LAST if r == ROUNDS - 1 else CH_HEADS)
                if r == TABLE_ROUND:
                    finish_tables()
                quantize("r", r)
                if r >= X_ROUND:
                    flush_products()
                if closing:
                    turn_plain(r)
                if not v_nope:
                    quantize("k", r)
                    if r >= X_ROUND:
                        flush_products()
